import numpy as np
import ml_dtypes


def mxq(x, axis, fmt="e4m3"):
    dtype, down = {"e4m3": (ml_dtypes.float8_e4m3fn, 7), "e5m2": (ml_dtypes.float8_e5m2, 14)}[fmt]
    v = np.moveaxis(np.asarray(x, np.float32).astype(ml_dtypes.bfloat16).astype(np.float64), axis, -1)
    blocks = v.reshape(v.shape[:-1] + (-1, 32))
    amax = np.abs(blocks).max(-1, keepdims=True)
    byte = np.maximum(np.where(amax > 0, np.frexp(amax)[1] - 1 + 127, 0) - down, 1)
    scale = np.exp2(byte - 127.0)
    codes = (blocks / scale).astype(np.float32).astype(dtype).astype(np.float64)
    return np.moveaxis((codes * scale).reshape(v.shape), -1, axis)


WIDE = False


def mx_kscale(k):
    if not WIDE:
        return np.ones(k)
    levels = np.array([10, -10, 5, -5, 0])
    a = np.random.permutation(np.resize(levels, k // 512 * 4)).reshape(k // 512, 4)
    idx = np.arange(k)
    return np.exp2(a[idx // 512, idx % 128 // 32])


BF16 = ml_dtypes.bfloat16


def bf(x):
    return np.asarray(x, np.float32).astype(BF16)


def f64(x):
    return np.asarray(x).astype(np.float64)


B, S, D = 4, 1024, 512
ALPHA = 1.0
BETA = 2.0
GAMMA = 1.5
TEMPERATURE = 1.0


def position_matrix(L):
    idx = np.arange(L, dtype=np.float64)
    dist = np.abs(idx[:, None] - idx[None, :]) / L
    base = np.exp(-BETA * dist)
    return ALPHA * (1.0 + GAMMA * base) / (1.0 + GAMMA)


def setup_inputs():
    s = mx_kscale(D)
    return {"q": bf(np.random.standard_normal((B, S, D)) * 1.5 * s),
            "k": bf(np.random.standard_normal((B, S, D)) * 1.5 / s),
            "v": bf(np.random.standard_normal((B, S, D)) * 1.5)}


def reference(q, k, v):
    scores = (mxq(f64(q), 2, "e4m3") @ mxq(f64(k), 2, "e4m3").transpose(0, 2, 1)) / np.sqrt(D)
    pw = position_matrix(S)
    scores = scores * pw[None, :, :] / TEMPERATURE
    e = np.exp(scores - scores.max(-1, keepdims=True))
    attn = e / e.sum(-1, keepdims=True)
    ctx = mxq(attn, 2, "e4m3") @ mxq(f64(v), 1, "e4m3")
    return ctx, attn

@@ -1,0 +1,329 @@
+from contextlib import ExitStack
+import math
+
+import concourse.bass as bass
+import concourse.mybir as mybir
+import concourse.tile as tile
+from concourse.masks import make_identity
+
+FP8X4 = mybir.dt.float8_e4m3fn_x4
+F32 = mybir.dt.float32
+BF16 = mybir.dt.bfloat16
+U32 = mybir.dt.uint32
+U8 = mybir.dt.uint8
+I32 = mybir.dt.int32
+ACT = mybir.ActivationFunctionType
+ALU = mybir.AluOpType
+AX = mybir.AxisListType
+
+B = 4
+S = 1024
+D = 512
+ALPHA = 1.0
+BETA = 2.0
+GAMMA = 1.5
+TEMPERATURE = 1.0
+P = 128
+NT = S // P
+TILES = B * NT
+FLOPS = 2 * 2 * B * S * S * D
+
+PINNED = False
+V_PREP_OUT = (1, 4, 6)
+
+
+def tile_positionawareattention_pa_t_kernel(tc, q, k, v, out_0, out_1):
+    nc = tc.nc
+    with ExitStack() as ctx:
+        if PINNED:
+            ctx.enter_context(tc.manual_schedule())
+        const = ctx.enter_context(tc.tile_pool(name="const", bufs=1))
+        raw = ctx.enter_context(tc.tile_pool(name="raw", bufs=1))
+        words = ctx.enter_context(tc.tile_pool(name="words", bufs=2))
+        stage = ctx.enter_context(tc.tile_pool(name="stage", bufs=3))
+        work = ctx.enter_context(tc.tile_pool(name="work", bufs=3))
+        small = ctx.enter_context(tc.tile_pool(name="small", bufs=4))
+        psum = ctx.enter_context(tc.psum_pool(name="psum", bufs=1))
+
+        q_raw, k_raw, v_raw = [], [], []
+        for b in range(B):
+            q_raw.append(raw.tile([P, NT * D], BF16, name="q_raw%d" % b, tag="q_raw%d" % b))
+            k_raw.append(raw.tile([P, NT * D], BF16, name="k_raw%d" % b, tag="k_raw%d" % b))
+            v_raw.append(raw.tile([P, NT * D], BF16, name="v_raw%d" % b, tag="v_raw%d" % b))
+
+        def load(dst, src, t0, t1):
+            nc.sync.dma_start(
+                out=dst[:, t0 * D : t1 * D].rearrange("p (t d) -> p t d", d=D),
+                in_=src[:, t0:t1, :],
+            )
+
+        def q_view(b):
+            return q[b].rearrange("(p t) d -> p t d", t=NT)
+
+        def k_view(b):
+            return k[b].rearrange("(t p) d -> p t d", p=P)
+
+        def v_view(b):
+            return v[b].rearrange("(t p) d -> p t d", p=P)
+
+        load(k_raw[0], k_view(0), 0, 4)
+        load(q_raw[0], q_view(0), 0, 4)
+        load(k_raw[0], k_view(0), 4, 8)
+        load(q_raw[0], q_view(0), 4, 8)
+        load(v_raw[0], v_view(0), 0, 8)
+        for b in range(1, B):
+            load(k_raw[b], k_view(b), 0, 8)
+            load(q_raw[b], q_view(b), 0, 8)
+            load(v_raw[b], v_view(b), 0, 8)
+
+        ident = const.tile([P, P], F32, name="ident", tag="ident")
+        make_identity(nc, ident[:])
+
+        TW = S + NT
+        d_hi_i = const.tile([P, TW // NT], I32, name="d_hi_i", tag="d_hi_i")
+        d_lo_i = const.tile([P, NT], I32, name="d_lo_i", tag="d_lo_i")
+        nc.gpsimd.iota(d_hi_i[:], pattern=[[-NT, TW // NT]], base=NT - 1, channel_multiplier=NT)
+        nc.gpsimd.iota(d_lo_i[:], pattern=[[1, NT]], base=0, channel_multiplier=0)
+        d_hi = const.tile([P, TW // NT], F32, name="d_hi", tag="d_hi")
+        d_lo = const.tile([P, NT], F32, name="d_lo", tag="d_lo")
+        nc.vector.tensor_copy(out=d_hi[:], in_=d_hi_i[:])
+        nc.vector.tensor_copy(out=d_lo[:], in_=d_lo_i[:])
+        dist = const.tile([P, TW], F32, name="dist", tag="dist")
+        nc.vector.tensor_tensor(
+            out=dist[:].rearrange("p (a c) -> p a c", c=NT),
+            in0=d_hi[:].unsqueeze(2).to_broadcast([P, TW // NT, NT]),
+            in1=d_lo[:].unsqueeze(1).to_broadcast([P, TW // NT, NT]),
+            op=ALU.subtract,
+        )
+        nc.scalar.activation(out=dist[:], in_=dist[:], func=ACT.Abs)
+        decay = const.tile([P, TW], F32, name="decay", tag="decay")
+        nc.scalar.activation(out=decay[:], in_=dist[:], func=ACT.Exp, scale=-BETA / S)
+        neg_pw = const.tile([P, TW], F32, name="neg_pw", tag="neg_pw")
+        unit_w = ALPHA / ((1.0 + GAMMA) * math.sqrt(D) * TEMPERATURE)
+        nc.vector.tensor_scalar(
+            out=neg_pw[:], in0=decay[:], scalar1=-GAMMA * unit_w, scalar2=-unit_w,
+            op0=ALU.mult, op1=ALU.add,
+        )
+
+        qw, qs, kw, ks, vw, vs = {}, {}, {}, {}, {}, {}
+        grouped = {}
+
+
+        def prep_transpose(b, u, tag):
+            src = (k_raw[b] if u < 4 else q_raw[b])[:].bitcast(F32)
+            t0 = 2 * (u % 4)
+            bank = psum.tile([P, 512], F32, name="prep_ps", tag=tag, bufs=(4 if tag == "score" else 1))
+            for s in range(2):
+                for h in range(2):
+                    col = (t0 + s) * (D // 2) + h * P
+                    nc.tensor.transpose(
+                        bank[:, (2 * s + h) * P : (2 * s + h + 1) * P], src[:, col : col + P], ident[:]
+                    )
+            return bank
+
+        def prep_out(b, u, bank, on_vector):
+            g = stage.tile([P, 1024], BF16, name="grouped", tag="grouped", align_bytes=64)
+            dst = g[:].bitcast(F32).rearrange("p (s r h) -> p s r h", s=2, h=2)
+            src = bank[:].rearrange("p (s h r) -> p s r h", s=2, h=2)
+            if on_vector:
+                nc.vector.tensor_copy(out=dst, in_=src)
+            else:
+                nc.scalar.copy(out=dst, in_=src)
+            grouped[(b, u)] = g
+
+        def prep_quant(b, u):
+            g = grouped[(b, u)]
+            c0 = 256 * (u % 4)
+            if u == 0:
+                kw[b] = words.tile([P, S], U32, name="kw", tag="kw", align_bytes=64)
+                ks[b] = words.tile([P, S], U8, name="ks", tag="ks", align_bytes=64)
+            if u == 4:
+                qw[b] = words.tile([P, S], U32, name="qw", tag="qw", align_bytes=64)
+                qs[b] = words.tile([P, S], U8, name="qs", tag="qs", align_bytes=64)
+            w, sc = (kw[b], ks[b]) if u < 4 else (qw[b], qs[b])
+            nc.vector.quantize_mx(
+                out=w[:, c0 : c0 + 256].bitcast(FP8X4), scales=sc[:, c0 : c0 + 256], in_=g[:]
+            )
+
+        v_grouped = {}
+
+        def v_regroup(b, g):
+            vg = stage.tile([P, 4 * D], BF16, name="v_grouped", tag="v_grouped", bufs=2, align_bytes=64)
+            nc.gpsimd.tensor_scalar(
+                out=vg[:].rearrange("p (c i t) -> p c t i", i=4, t=4),
+                in0=v_raw[b][:, g * 4 * D : (g + 1) * 4 * D].rearrange("p (t c i) -> p c t i", t=4, i=4),
+                scalar1=1.0, scalar2=0.0, op0=ALU.mult, op1=ALU.add,
+            )
+            v_grouped[(b, g)] = vg
+
+        def v_quant(b, g):
+            vg = v_grouped[(b, g)]
+            if g == 0:
+                vw[b] = words.tile([P, 2 * D], U32, name="vw", tag="vw", align_bytes=64)
+                vs[b] = words.tile([P, 2 * D], U8, name="vs", tag="vs", align_bytes=64)
+            nc.vector.quantize_mx(
+                out=vw[b][:, g * D : (g + 1) * D].bitcast(FP8X4),
+                scales=vs[b][:, g * D : (g + 1) * D],
+                in_=vg[:],
+            )
+
+        score_ps, x_sb, neg_max, row_sum, attn_sb, at_ps, at_grouped = {}, {}, {}, {}, {}, {}, {}
+        at_words, at_scales, ctx_ps, ctx_sb = {}, {}, {}, {}
+        attn_out = [out_1[b].rearrange("(p t) j -> p t j", t=NT) for b in range(B)]
+        ctx_out = [out_0[b].rearrange("(p t) d -> p t d", t=NT) for b in range(B)]
+
+        def qk(n):
+            b, t = divmod(n, NT)
+            for h in range(2):
+                ps = psum.tile([P, 512], F32, name="score_ps", tag="score", bufs=4)
+                nc.tensor.matmul_mx(
+                    out=ps[:],
+                    lhsT=qw[b][:, t * P : (t + 1) * P].bitcast(FP8X4),
+                    lhsT_scale=qs[b][:, t * P : (t + 1) * P],
+                    rhs=kw[b][:, h * 512 : (h + 1) * 512].bitcast(FP8X4),
+                    rhs_scale=ks[b][:, h * 512 : (h + 1) * 512],
+                    start=True, stop=True,
+                )
+                score_ps[(n, h)] = ps
+
+        def weigh_and_max(n):
+            t = n % NT
+            x = work.tile([P, S], F32, name="x_sb", tag="x_sb")
+            for h in range(2):
+                c0 = NT - 1 - t + h * 512
+                nc.vector.tensor_tensor(
+                    out=x[:, h * 512 : (h + 1) * 512], in0=score_ps[(n, h)][:],
+                    in1=neg_pw[:, c0 : c0 + 512], op=ALU.mult,
+                )
+            m = small.tile([P, 1], F32, name="neg_max", tag="neg_max")
+            nc.vector.tensor_reduce(out=m[:], in_=x[:], axis=AX.X, op=ALU.min)
+            x_sb[n], neg_max[n] = x, m
+
+        def exponent(n):
+            if n % 2 == 0:
+                attn_sb[n // 2] = work.tile([P, 2 * S], F32, name="attn_sb", tag="attn_sb", bufs=4)
+            a = attn_sb[n // 2][:, (n % 2) * S : (n % 2 + 1) * S]
+            sm = small.tile([P, 1], F32, name="row_sum", tag="row_sum")
+            nc.scalar.activation(
+                out=a, in_=x_sb[n][:], func=ACT.Exp, bias=neg_max[n][:], scale=-1.0,
+                accum_out=sm[:],
+            )
+            row_sum[n] = sm
+
+        def normalise(n):
+            b, t = divmod(n, NT)
+            r = small.tile([P, 1], F32, name="recip", tag="recip")
+            nc.vector.reciprocal(out=r[:], in_=row_sum[n][:])
+            a = attn_sb[n // 2][:, (n % 2) * S : (n % 2 + 1) * S]
+            nc.gpsimd.tensor_scalar(
+                out=a, in0=a, scalar1=r[:], scalar2=0.0, op0=ALU.mult, op1=ALU.add
+            )
+            if n % 2 == 1:
+                nc.sync.dma_start(
+                    out=attn_out[b][:, t - 1 : t + 1, :],
+                    in_=attn_sb[n // 2][:].rearrange("p (t j) -> p t j", t=2),
+                )
+
+        def transpose_attn(n):
+            a = attn_sb[n // 2]
+            for g in range(2):
+                ps = psum.tile([P, 512], F32, name="at_ps", tag="at_ps", bufs=2)
+                for c in range(4):
+                    col = (n % 2) * S + (4 * g + c) * P
+                    nc.tensor.transpose(ps[:, c * P : (c + 1) * P], a[:, col : col + P], ident[:])
+                at_ps[(n, g)] = ps
+            if n % 2 == 1:
+                attn_sb[n // 2]
+
+        def regroup_attn(n):
+            gr = stage.tile([P, 1024], BF16, name="at_grouped", tag="at_grouped", align_bytes=64)
+            for g in range(2):
+                nc.scalar.copy(
+                    out=gr[:, g * 512 : (g + 1) * 512].rearrange("p (r c) -> p r c", c=4),
+                    in_=at_ps[(n, g)][:].rearrange("p (c r) -> p r c", c=4),
+                )
+            at_grouped[n] = gr
+
+        def quantise_attn(n):
+            w = stage.tile([P, 256], U32, name="at_words", tag="at_words", align_bytes=64)
+            sc = stage.tile([P, 256], U8, name="at_scales", tag="at_scales", align_bytes=64)
+            nc.vector.quantize_mx(out=w[:].bitcast(FP8X4), scales=sc[:], in_=at_grouped[n][:])
+            at_words[n], at_scales[n] = w, sc
+
+        def av(n):
+            b = n // NT
+            ps = psum.tile([P, 512], F32, name="ctx_ps", tag="ctx_ps", bufs=1)
+            w, sc = at_words[n], at_scales[n]
+            for g in range(2):
+                nc.tensor.matmul_mx(
+                    out=ps[:],
+                    lhsT=w[:, g * P : (g + 1) * P].bitcast(FP8X4),
+                    lhsT_scale=sc[:, g * P : (g + 1) * P],
+                    rhs=vw[b][:, g * D : (g + 1) * D].bitcast(FP8X4),
+                    rhs_scale=vs[b][:, g * D : (g + 1) * D],
+                    start=(g == 0), stop=(g == 1),
+                )
+            ctx_ps[n] = ps
+
+        def ctx_store(n):
+            b, t = divmod(n, NT)
+            if n % 2 == 0:
+                ctx_sb[n // 2] = work.tile([P, 2 * D], F32, name="ctx_sb", tag="ctx_sb")
+            c = ctx_sb[n // 2]
+            nc.scalar.copy(out=c[:, (n % 2) * D : (n % 2 + 1) * D], in_=ctx_ps[n][:])
+            if n % 2 == 1:
+                nc.sync.dma_start(
+                    out=ctx_out[b][:, t - 1 : t + 1, :],
+                    in_=ctx_sb[n // 2][:].rearrange("p (t d) -> p t d", t=2),
+                )
+
+        order0 = [0, 1, 4, 2, 3, 5, 6, 7]
+        banks = {}
+        for i, u in enumerate(order0):
+            banks[u] = prep_transpose(0, u, "score")
+            prep_out(0, u, banks[u], on_vector=(i % 2 == 0))
+            if i >= 1:
+                prep_quant(0, order0[i - 1])
+        prep_quant(0, order0[-1])
+        v_regroup(0, 0)
+        v_regroup(0, 1)
+        qk(0)
+
+        for step in range(TILES + 3):
+            b_next = step // NT + 1
+            u = step % NT
+            prep = b_next < B and step < TILES
+            if 0 <= step - 3 < TILES:
+                av(step - 3)
+            if step + 1 < TILES:
+                qk(step + 1)
+            if step < TILES:
+                weigh_and_max(step)
+            if 0 <= step - 1 < TILES:
+                exponent(step - 1)
+            if 0 <= step - 3 < TILES:
+                ctx_store(step - 3)
+            if 0 <= step - 1 < TILES:
+                normalise(step - 1)
+            if 0 <= step - 2 < TILES:
+                transpose_attn(step - 2)
+            if prep:
+                bank = prep_transpose(b_next, u, "prep")
+            if 0 <= step - 2 < TILES:
+                regroup_attn(step - 2)
+            if prep:
+                prep_out(b_next, u, bank, on_vector=(u in V_PREP_OUT))
+                if u in (2, 4):
+                    v_regroup(b_next, (u - 2) // 2)
+            if step == 0:
+                v_quant(0, 0)
+            if step == 1:
+                v_quant(0, 1)
+            if 1 <= u and b_next < B and step < TILES:
+                prep_quant(b_next, u - 1)
+            if u == 0 and 1 <= step // NT < B and step < TILES:
+                prep_quant(step // NT, NT - 1)
+            if prep and u in (5, 7):
+                v_quant(b_next, (u - 5) // 2)
+            if 0 <= step - 2 < TILES:
+                quantise_attn(step - 2)

@@ -1,9 +1,7 @@
 from contextlib import ExitStack
 import math
 
-import concourse.bass as bass
 import concourse.mybir as mybir
-import concourse.tile as tile
 from concourse.masks import make_identity
 
 FP8X4 = mybir.dt.float8_e4m3fn_x4
@@ -26,10 +24,10 @@ TEMPERATURE = 1.0
 P = 128
 NT = S // P
 TILES = B * NT
+BANK = 512
 FLOPS = 2 * 2 * B * S * S * D
 
-PINNED = False
-V_PREP_OUT = (1, 4, 6)
+PINNED = True
 
 
 def tile_positionawareattention_pa_t_kernel(tc, q, k, v, out_0, out_1):
@@ -57,33 +55,28 @@ def tile_positionawareattention_pa_t_kernel(tc, q, k, v, out_0, out_1):
                 in_=src[:, t0:t1, :],
             )
 
-        def q_view(b):
-            return q[b].rearrange("(p t) d -> p t d", t=NT)
+        q_view = [q[b].rearrange("(p t) d -> p t d", t=NT) for b in range(B)]
+        k_view = [k[b].rearrange("(t p) d -> p t d", p=P) for b in range(B)]
+        v_view = [v[b].rearrange("(t p) d -> p t d", p=P) for b in range(B)]
 
-        def k_view(b):
-            return k[b].rearrange("(t p) d -> p t d", p=P)
-
-        def v_view(b):
-            return v[b].rearrange("(t p) d -> p t d", p=P)
-
-        load(k_raw[0], k_view(0), 0, 4)
-        load(q_raw[0], q_view(0), 0, 4)
-        load(k_raw[0], k_view(0), 4, 8)
-        load(q_raw[0], q_view(0), 4, 8)
-        load(v_raw[0], v_view(0), 0, 8)
+        load(k_raw[0], k_view[0], 0, 4)
+        load(q_raw[0], q_view[0], 0, 4)
+        load(k_raw[0], k_view[0], 4, 8)
+        load(q_raw[0], q_view[0], 4, 8)
+        load(v_raw[0], v_view[0], 0, 4)
+        load(v_raw[0], v_view[0], 4, 8)
         for b in range(1, B):
-            load(k_raw[b], k_view(b), 0, 8)
-            load(q_raw[b], q_view(b), 0, 8)
-            load(v_raw[b], v_view(b), 0, 8)
-
-        ident = const.tile([P, P], F32, name="ident", tag="ident")
-        make_identity(nc, ident[:])
+            load(k_raw[b], k_view[b], 0, 8)
+            load(q_raw[b], q_view[b], 0, 8)
+            load(v_raw[b], v_view[b], 0, 8)
 
         TW = S + NT
         d_hi_i = const.tile([P, TW // NT], I32, name="d_hi_i", tag="d_hi_i")
         d_lo_i = const.tile([P, NT], I32, name="d_lo_i", tag="d_lo_i")
         nc.gpsimd.iota(d_hi_i[:], pattern=[[-NT, TW // NT]], base=NT - 1, channel_multiplier=NT)
         nc.gpsimd.iota(d_lo_i[:], pattern=[[1, NT]], base=0, channel_multiplier=0)
+        ident = const.tile([P, P], F32, name="ident", tag="ident")
+        make_identity(nc, ident[:])
         d_hi = const.tile([P, TW // NT], F32, name="d_hi", tag="d_hi")
         d_lo = const.tile([P, NT], F32, name="d_lo", tag="d_lo")
         nc.vector.tensor_copy(out=d_hi[:], in_=d_hi_i[:])
@@ -100,39 +93,43 @@ def tile_positionawareattention_pa_t_kernel(tc, q, k, v, out_0, out_1):
         nc.scalar.activation(out=decay[:], in_=dist[:], func=ACT.Exp, scale=-BETA / S)
         neg_pw = const.tile([P, TW], F32, name="neg_pw", tag="neg_pw")
         unit_w = ALPHA / ((1.0 + GAMMA) * math.sqrt(D) * TEMPERATURE)
-        nc.vector.tensor_scalar(
-            out=neg_pw[:], in0=decay[:], scalar1=-GAMMA * unit_w, scalar2=-unit_w,
-            op0=ALU.mult, op1=ALU.add,
-        )
+
+        def finish_table():
+            nc.vector.tensor_scalar(
+                out=neg_pw[:], in0=decay[:], scalar1=-GAMMA * unit_w, scalar2=-unit_w,
+                op0=ALU.mult, op1=ALU.add,
+            )
 
         qw, qs, kw, ks, vw, vs = {}, {}, {}, {}, {}, {}
-        grouped = {}
+        prep_ps, grouped, v_grouped = {}, {}, {}
 
+        def copy_out(on_vector, out, in_):
+            if on_vector:
+                nc.vector.tensor_copy(out=out, in_=in_)
+            else:
+                nc.scalar.copy(out=out, in_=in_)
 
-        def prep_transpose(b, u, tag):
+        def prep_transpose(b, u, tag, bufs):
             src = (k_raw[b] if u < 4 else q_raw[b])[:].bitcast(F32)
-            t0 = 2 * (u % 4)
-            bank = psum.tile([P, 512], F32, name="prep_ps", tag=tag, bufs=(4 if tag == "score" else 1))
+            bank = psum.tile([P, BANK], F32, name="prep_ps", tag=tag, bufs=bufs)
             for s in range(2):
                 for h in range(2):
-                    col = (t0 + s) * (D // 2) + h * P
+                    col = (2 * (u % 4) + s) * (D // 2) + h * P
                     nc.tensor.transpose(
                         bank[:, (2 * s + h) * P : (2 * s + h + 1) * P], src[:, col : col + P], ident[:]
                     )
-            return bank
+            prep_ps[(b, u)] = bank
 
-        def prep_out(b, u, bank, on_vector):
+        def prep_out(b, u, on_vector):
             g = stage.tile([P, 1024], BF16, name="grouped", tag="grouped", align_bytes=64)
-            dst = g[:].bitcast(F32).rearrange("p (s r h) -> p s r h", s=2, h=2)
-            src = bank[:].rearrange("p (s h r) -> p s r h", s=2, h=2)
-            if on_vector:
-                nc.vector.tensor_copy(out=dst, in_=src)
-            else:
-                nc.scalar.copy(out=dst, in_=src)
+            copy_out(
+                on_vector,
+                g[:].bitcast(F32).rearrange("p (s r h) -> p s r h", s=2, h=2),
+                prep_ps[(b, u)][:].rearrange("p (s h r) -> p s r h", s=2, h=2),
+            )
             grouped[(b, u)] = g
 
         def prep_quant(b, u):
-            g = grouped[(b, u)]
             c0 = 256 * (u % 4)
             if u == 0:
                 kw[b] = words.tile([P, S], U32, name="kw", tag="kw", align_bytes=64)
@@ -142,10 +139,9 @@ def tile_positionawareattention_pa_t_kernel(tc, q, k, v, out_0, out_1):
                 qs[b] = words.tile([P, S], U8, name="qs", tag="qs", align_bytes=64)
             w, sc = (kw[b], ks[b]) if u < 4 else (qw[b], qs[b])
             nc.vector.quantize_mx(
-                out=w[:, c0 : c0 + 256].bitcast(FP8X4), scales=sc[:, c0 : c0 + 256], in_=g[:]
+                out=w[:, c0 : c0 + 256].bitcast(FP8X4), scales=sc[:, c0 : c0 + 256],
+                in_=grouped[(b, u)][:],
             )
-
-        v_grouped = {}
 
         def v_regroup(b, g):
             vg = stage.tile([P, 4 * D], BF16, name="v_grouped", tag="v_grouped", bufs=2, align_bytes=64)
@@ -157,14 +153,13 @@ def tile_positionawareattention_pa_t_kernel(tc, q, k, v, out_0, out_1):
             v_grouped[(b, g)] = vg
 
         def v_quant(b, g):
-            vg = v_grouped[(b, g)]
             if g == 0:
                 vw[b] = words.tile([P, 2 * D], U32, name="vw", tag="vw", align_bytes=64)
                 vs[b] = words.tile([P, 2 * D], U8, name="vs", tag="vs", align_bytes=64)
             nc.vector.quantize_mx(
                 out=vw[b][:, g * D : (g + 1) * D].bitcast(FP8X4),
                 scales=vs[b][:, g * D : (g + 1) * D],
-                in_=vg[:],
+                in_=v_grouped[(b, g)][:],
             )
 
         score_ps, x_sb, neg_max, row_sum, attn_sb, at_ps, at_grouped = {}, {}, {}, {}, {}, {}, {}
@@ -175,13 +170,13 @@ def tile_positionawareattention_pa_t_kernel(tc, q, k, v, out_0, out_1):
         def qk(n):
             b, t = divmod(n, NT)
             for h in range(2):
-                ps = psum.tile([P, 512], F32, name="score_ps", tag="score", bufs=4)
+                ps = psum.tile([P, BANK], F32, name="score_ps", tag="score", bufs=4)
                 nc.tensor.matmul_mx(
                     out=ps[:],
                     lhsT=qw[b][:, t * P : (t + 1) * P].bitcast(FP8X4),
                     lhsT_scale=qs[b][:, t * P : (t + 1) * P],
-                    rhs=kw[b][:, h * 512 : (h + 1) * 512].bitcast(FP8X4),
-                    rhs_scale=ks[b][:, h * 512 : (h + 1) * 512],
+                    rhs=kw[b][:, h * BANK : (h + 1) * BANK].bitcast(FP8X4),
+                    rhs_scale=ks[b][:, h * BANK : (h + 1) * BANK],
                     start=True, stop=True,
                 )
                 score_ps[(n, h)] = ps
@@ -190,10 +185,10 @@ def tile_positionawareattention_pa_t_kernel(tc, q, k, v, out_0, out_1):
             t = n % NT
             x = work.tile([P, S], F32, name="x_sb", tag="x_sb")
             for h in range(2):
-                c0 = NT - 1 - t + h * 512
+                c0 = NT - 1 - t + h * BANK
                 nc.vector.tensor_tensor(
-                    out=x[:, h * 512 : (h + 1) * 512], in0=score_ps[(n, h)][:],
-                    in1=neg_pw[:, c0 : c0 + 512], op=ALU.mult,
+                    out=x[:, h * BANK : (h + 1) * BANK], in0=score_ps[(n, h)][:],
+                    in1=neg_pw[:, c0 : c0 + BANK], op=ALU.mult,
                 )
             m = small.tile([P, 1], F32, name="neg_max", tag="neg_max")
             nc.vector.tensor_reduce(out=m[:], in_=x[:], axis=AX.X, op=ALU.min)
@@ -202,11 +197,10 @@ def tile_positionawareattention_pa_t_kernel(tc, q, k, v, out_0, out_1):
         def exponent(n):
             if n % 2 == 0:
                 attn_sb[n // 2] = work.tile([P, 2 * S], F32, name="attn_sb", tag="attn_sb", bufs=4)
-            a = attn_sb[n // 2][:, (n % 2) * S : (n % 2 + 1) * S]
             sm = small.tile([P, 1], F32, name="row_sum", tag="row_sum")
             nc.scalar.activation(
-                out=a, in_=x_sb[n][:], func=ACT.Exp, bias=neg_max[n][:], scale=-1.0,
-                accum_out=sm[:],
+                out=attn_sb[n // 2][:, (n % 2) * S : (n % 2 + 1) * S], in_=x_sb[n][:], func=ACT.Exp,
+                bias=neg_max[n][:], scale=-1.0, accum_out=sm[:],
             )
             row_sum[n] = sm
 
@@ -225,21 +219,20 @@ def tile_positionawareattention_pa_t_kernel(tc, q, k, v, out_0, out_1):
                 )
 
         def transpose_attn(n):
-            a = attn_sb[n // 2]
             for g in range(2):
-                ps = psum.tile([P, 512], F32, name="at_ps", tag="at_ps", bufs=2)
+                ps = psum.tile([P, BANK], F32, name="at_ps", tag="at_ps", bufs=2)
                 for c in range(4):
                     col = (n % 2) * S + (4 * g + c) * P
-                    nc.tensor.transpose(ps[:, c * P : (c + 1) * P], a[:, col : col + P], ident[:])
+                    nc.tensor.transpose(
+                        ps[:, c * P : (c + 1) * P], attn_sb[n // 2][:, col : col + P], ident[:]
+                    )
                 at_ps[(n, g)] = ps
-            if n % 2 == 1:
-                attn_sb[n // 2]
 
         def regroup_attn(n):
             gr = stage.tile([P, 1024], BF16, name="at_grouped", tag="at_grouped", align_bytes=64)
             for g in range(2):
                 nc.scalar.copy(
-                    out=gr[:, g * 512 : (g + 1) * 512].rearrange("p (r c) -> p r c", c=4),
+                    out=gr[:, g * BANK : (g + 1) * BANK].rearrange("p (r c) -> p r c", c=4),
                     in_=at_ps[(n, g)][:].rearrange("p (c r) -> p r c", c=4),
                 )
             at_grouped[n] = gr
@@ -252,78 +245,79 @@ def tile_positionawareattention_pa_t_kernel(tc, q, k, v, out_0, out_1):
 
         def av(n):
             b = n // NT
-            ps = psum.tile([P, 512], F32, name="ctx_ps", tag="ctx_ps", bufs=1)
-            w, sc = at_words[n], at_scales[n]
+            ps = psum.tile([P, BANK], F32, name="ctx_ps", tag="ctx_ps", bufs=1)
             for g in range(2):
                 nc.tensor.matmul_mx(
                     out=ps[:],
-                    lhsT=w[:, g * P : (g + 1) * P].bitcast(FP8X4),
-                    lhsT_scale=sc[:, g * P : (g + 1) * P],
+                    lhsT=at_words[n][:, g * P : (g + 1) * P].bitcast(FP8X4),
+                    lhsT_scale=at_scales[n][:, g * P : (g + 1) * P],
                     rhs=vw[b][:, g * D : (g + 1) * D].bitcast(FP8X4),
                     rhs_scale=vs[b][:, g * D : (g + 1) * D],
                     start=(g == 0), stop=(g == 1),
                 )
             ctx_ps[n] = ps
 
-        def ctx_store(n):
+        def ctx_store(n, on_vector):
             b, t = divmod(n, NT)
             if n % 2 == 0:
                 ctx_sb[n // 2] = work.tile([P, 2 * D], F32, name="ctx_sb", tag="ctx_sb")
-            c = ctx_sb[n // 2]
-            nc.scalar.copy(out=c[:, (n % 2) * D : (n % 2 + 1) * D], in_=ctx_ps[n][:])
+            copy_out(on_vector, ctx_sb[n // 2][:, (n % 2) * D : (n % 2 + 1) * D], ctx_ps[n][:])
             if n % 2 == 1:
                 nc.sync.dma_start(
                     out=ctx_out[b][:, t - 1 : t + 1, :],
                     in_=ctx_sb[n // 2][:].rearrange("p (t d) -> p t d", t=2),
                 )
 
-        order0 = [0, 1, 4, 2, 3, 5, 6, 7]
-        banks = {}
-        for i, u in enumerate(order0):
-            banks[u] = prep_transpose(0, u, "score")
-            prep_out(0, u, banks[u], on_vector=(i % 2 == 0))
+        first = [0, 1, 4, 5, 2, 3]
+        for i, u in enumerate(first):
+            prep_transpose(0, u, "score" if i < 4 else "at_ps", 4 if i < 4 else 2)
+        for i, u in enumerate(first):
+            prep_out(0, u, on_vector=(i % 2 == 0))
+            if i == 3:
+                finish_table()
             if i >= 1:
-                prep_quant(0, order0[i - 1])
-        prep_quant(0, order0[-1])
+                prep_quant(0, first[i - 1])
+        prep_quant(0, first[-1])
         v_regroup(0, 0)
         v_regroup(0, 1)
         qk(0)
 
+        units = [(0, 6), (0, 7)] + [(b, u) for b in range(1, B) for u in range(8)]
+
+        def live(n):
+            return 0 <= n < TILES
+
         for step in range(TILES + 3):
-            b_next = step // NT + 1
-            u = step % NT
-            prep = b_next < B and step < TILES
-            if 0 <= step - 3 < TILES:
-                av(step - 3)
-            if step + 1 < TILES:
+            odd = step % 2 == 1
+            b_v, s_v = divmod(step + 4, NT)
+            b_w, s_w = divmod(step + 2, NT)
+            if live(step - 3):
+                quantise_attn(step - 3)
+            if 1 <= step <= len(units):
+                prep_quant(units[step - 1][0], units[step - 1][1])
+            if step in (0, 1):
+                v_quant(0, step)
+            if 1 <= b_w < B and s_w in (0, 2):
+                v_quant(b_w, s_w // 2)
+            if live(step + 1):
                 qk(step + 1)
-            if step < TILES:
+            if live(step - 3):
+                av(step - 3)
+            if live(step):
                 weigh_and_max(step)
-            if 0 <= step - 1 < TILES:
+            if live(step - 1):
                 exponent(step - 1)
-            if 0 <= step - 3 < TILES:
-                ctx_store(step - 3)
-            if 0 <= step - 1 < TILES:
+            if live(step - 3):
+                ctx_store(step - 3, on_vector=(odd and step >= len(units)))
+            if live(step - 1):
                 normalise(step - 1)
-            if 0 <= step - 2 < TILES:
+            if 1 <= b_v < B and s_v in (0, 2):
+                v_regroup(b_v, s_v // 2)
+            if live(step - 2):
                 transpose_attn(step - 2)
-            if prep:
-                bank = prep_transpose(b_next, u, "prep")
-            if 0 <= step - 2 < TILES:
+            if step < len(units):
+                prep_transpose(units[step][0], units[step][1], "prep", 1)
+            if live(step - 2):
                 regroup_attn(step - 2)
-            if prep:
-                prep_out(b_next, u, bank, on_vector=(u in V_PREP_OUT))
-                if u in (2, 4):
-                    v_regroup(b_next, (u - 2) // 2)
-            if step == 0:
-                v_quant(0, 0)
-            if step == 1:
-                v_quant(0, 1)
-            if 1 <= u and b_next < B and step < TILES:
-                prep_quant(b_next, u - 1)
-            if u == 0 and 1 <= step // NT < B and step < TILES:
-                prep_quant(step // NT, NT - 1)
-            if prep and u in (5, 7):
-                v_quant(b_next, (u - 5) // 2)
-            if 0 <= step - 2 < TILES:
-                quantise_attn(step - 2)
+            if step < len(units):
+                prep_out(units[step][0], units[step][1], on_vector=odd)

@@ -121,7 +121,7 @@ def tile_positionawareattention_pa_t_kernel(tc, q, k, v, out_0, out_1):
             prep_ps[(b, u)] = bank
 
         def prep_out(b, u, on_vector):
-            g = stage.tile([P, 1024], BF16, name="grouped", tag="grouped", align_bytes=64)
+            g = stage.tile([P, 1024], BF16, name="grouped", tag="grouped", bufs=4, align_bytes=64)
             copy_out(
                 on_vector,
                 g[:].bitcast(F32).rearrange("p (s r h) -> p s r h", s=2, h=2),
@@ -170,7 +170,7 @@ def tile_positionawareattention_pa_t_kernel(tc, q, k, v, out_0, out_1):
         def qk(n):
             b, t = divmod(n, NT)
             for h in range(2):
-                ps = psum.tile([P, BANK], F32, name="score_ps", tag="score", bufs=4)
+                ps = psum.tile([P, BANK], F32, name="score_ps", tag="score", bufs=5)
                 nc.tensor.matmul_mx(
                     out=ps[:],
                     lhsT=qw[b][:, t * P : (t + 1) * P].bitcast(FP8X4),
@@ -204,23 +204,26 @@ def tile_positionawareattention_pa_t_kernel(tc, q, k, v, out_0, out_1):
             )
             row_sum[n] = sm
 
-        def normalise(n):
+        def normalise(n, on_vector):
             b, t = divmod(n, NT)
             r = small.tile([P, 1], F32, name="recip", tag="recip")
             nc.vector.reciprocal(out=r[:], in_=row_sum[n][:])
             a = attn_sb[n // 2][:, (n % 2) * S : (n % 2 + 1) * S]
-            nc.gpsimd.tensor_scalar(
-                out=a, in0=a, scalar1=r[:], scalar2=0.0, op0=ALU.mult, op1=ALU.add
-            )
+            if on_vector:
+                nc.vector.tensor_scalar_mul(out=a, in0=a, scalar1=r[:])
+            else:
+                nc.gpsimd.tensor_scalar(
+                    out=a, in0=a, scalar1=r[:], scalar2=0.0, op0=ALU.mult, op1=ALU.add
+                )
             if n % 2 == 1:
                 nc.sync.dma_start(
                     out=attn_out[b][:, t - 1 : t + 1, :],
                     in_=attn_sb[n // 2][:].rearrange("p (t j) -> p t j", t=2),
                 )
 
-        def transpose_attn(n):
+        def transpose_attn(n, tag, bufs):
             for g in range(2):
-                ps = psum.tile([P, BANK], F32, name="at_ps", tag="at_ps", bufs=2)
+                ps = psum.tile([P, BANK], F32, name="at_ps", tag=tag, bufs=bufs)
                 for c in range(4):
                     col = (n % 2) * S + (4 * g + c) * P
                     nc.tensor.transpose(
@@ -228,12 +231,13 @@ def tile_positionawareattention_pa_t_kernel(tc, q, k, v, out_0, out_1):
                     )
                 at_ps[(n, g)] = ps
 
-        def regroup_attn(n):
+        def regroup_attn(n, shared):
             gr = stage.tile([P, 1024], BF16, name="at_grouped", tag="at_grouped", align_bytes=64)
             for g in range(2):
-                nc.scalar.copy(
-                    out=gr[:, g * BANK : (g + 1) * BANK].rearrange("p (r c) -> p r c", c=4),
-                    in_=at_ps[(n, g)][:].rearrange("p (c r) -> p r c", c=4),
+                copy_out(
+                    shared and g == 1,
+                    gr[:, g * BANK : (g + 1) * BANK].rearrange("p (r c) -> p r c", c=4),
+                    at_ps[(n, g)][:].rearrange("p (c r) -> p r c", c=4),
                 )
             at_grouped[n] = gr
 
@@ -245,7 +249,7 @@ def tile_positionawareattention_pa_t_kernel(tc, q, k, v, out_0, out_1):
 
         def av(n):
             b = n // NT
-            ps = psum.tile([P, BANK], F32, name="ctx_ps", tag="ctx_ps", bufs=1)
+            ps = psum.tile([P, BANK], F32, name="ctx_ps", tag="score", bufs=5)
             for g in range(2):
                 nc.tensor.matmul_mx(
                     out=ps[:],
@@ -270,7 +274,7 @@ def tile_positionawareattention_pa_t_kernel(tc, q, k, v, out_0, out_1):
 
         first = [0, 1, 4, 5, 2, 3]
         for i, u in enumerate(first):
-            prep_transpose(0, u, "score" if i < 4 else "at_ps", 4 if i < 4 else 2)
+            prep_transpose(0, u, "score" if i < 4 else "at_ps", 5 if i < 4 else 2)
         for i, u in enumerate(first):
             prep_out(0, u, on_vector=(i % 2 == 0))
             if i == 3:
@@ -282,42 +286,50 @@ def tile_positionawareattention_pa_t_kernel(tc, q, k, v, out_0, out_1):
         v_regroup(0, 1)
         qk(0)
 
-        units = [(0, 6), (0, 7)] + [(b, u) for b in range(1, B) for u in range(8)]
+        units = [(b, u) for b in range(1, B) for u in range(8)]
 
         def live(n):
             return 0 <= n < TILES
 
-        for step in range(TILES + 3):
-            odd = step % 2 == 1
-            b_v, s_v = divmod(step + 4, NT)
-            b_w, s_w = divmod(step + 2, NT)
-            if live(step - 3):
-                quantise_attn(step - 3)
-            if 1 <= step <= len(units):
-                prep_quant(units[step - 1][0], units[step - 1][1])
+        def unit(j):
+            return units[j] if 0 <= j < len(units) else None
+
+        for step in range(TILES + 8):
+            late = step >= TILES
+            if live(step - 2):
+                normalise(step - 2, on_vector=late)
+            if live(step - 4):
+                transpose_attn(step - 4, "score" if late else "at_ps", 5 if late else 2)
             if step in (0, 1):
-                v_quant(0, step)
-            if 1 <= b_w < B and s_w in (0, 2):
-                v_quant(b_w, s_w // 2)
+                prep_transpose(0, 6 + step, "at_ps", 2)
+            if unit(step):
+                prep_transpose(unit(step)[0], unit(step)[1], "prep", 1)
             if live(step + 1):
                 qk(step + 1)
-            if live(step - 3):
-                av(step - 3)
             if live(step):
                 weigh_and_max(step)
             if live(step - 1):
                 exponent(step - 1)
-            if live(step - 3):
-                ctx_store(step - 3, on_vector=(odd and step >= len(units)))
-            if live(step - 1):
-                normalise(step - 1)
-            if 1 <= b_v < B and s_v in (0, 2):
-                v_regroup(b_v, s_v // 2)
-            if live(step - 2):
-                transpose_attn(step - 2)
-            if step < len(units):
-                prep_transpose(units[step][0], units[step][1], "prep", 1)
-            if live(step - 2):
-                regroup_attn(step - 2)
-            if step < len(units):
-                prep_out(units[step][0], units[step][1], on_vector=odd)
+            if live(step - 7):
+                ctx_store(step - 7, on_vector=((step - 7) % 4 == 3))
+            if live(step - 6):
+                av(step - 6)
+            if live(step - 4):
+                regroup_attn(step - 4, shared=late)
+            if step in (0, 1):
+                prep_out(0, 6 + step, on_vector=False)
+            if unit(step):
+                prep_out(unit(step)[0], unit(step)[1], on_vector=False)
+            if live(step - 5):
+                quantise_attn(step - 5)
+            if unit(step - 1):
+                prep_quant(unit(step - 1)[0], unit(step - 1)[1])
+            if step in (1, 2):
+                prep_quant(0, 5 + step)
+            if step in (0, 1):
+                v_quant(0, step)
+            for b in range(1, B):
+                if step in (NT * b - 4, NT * b - 2):
+                    v_regroup(b, (step - NT * b + 4) // 2)
+                if step in (NT * b - 1, NT * b + 1):
+                    v_quant(b, (step - NT * b + 1) // 2)

@@ -28,6 +28,7 @@ BANK = 512
 FLOPS = 2 * 2 * B * S * S * D
 
 PINNED = True
+COUT_V = 0
 
 
 def tile_positionawareattention_pa_t_kernel(tc, q, k, v, out_0, out_1):
@@ -59,9 +60,12 @@ def tile_positionawareattention_pa_t_kernel(tc, q, k, v, out_0, out_1):
         k_view = [k[b].rearrange("(t p) d -> p t d", p=P) for b in range(B)]
         v_view = [v[b].rearrange("(t p) d -> p t d", p=P) for b in range(B)]
 
-        load(k_raw[0], k_view[0], 0, 4)
-        load(q_raw[0], q_view[0], 0, 4)
-        load(k_raw[0], k_view[0], 4, 8)
+        load(k_raw[0], k_view[0], 0, 2)
+        load(q_raw[0], q_view[0], 0, 2)
+        load(k_raw[0], k_view[0], 2, 4)
+        load(k_raw[0], k_view[0], 4, 6)
+        load(k_raw[0], k_view[0], 6, 8)
+        load(q_raw[0], q_view[0], 2, 4)
         load(q_raw[0], q_view[0], 4, 8)
         load(v_raw[0], v_view[0], 0, 4)
         load(v_raw[0], v_view[0], 4, 8)
@@ -143,23 +147,25 @@ def tile_positionawareattention_pa_t_kernel(tc, q, k, v, out_0, out_1):
                 in_=grouped[(b, u)][:],
             )
 
-        def v_regroup(b, g):
-            vg = stage.tile([P, 4 * D], BF16, name="v_grouped", tag="v_grouped", bufs=2, align_bytes=64)
+        def v_regroup(w):
+            b, g, c = w // 8, (w % 8) // 4, w % 4
+            vg = stage.tile([P, 4 * P], BF16, name="v_grouped", tag="v_grouped", bufs=5, align_bytes=64)
+            src = v_raw[b][:, g * 4 * D : (g + 1) * 4 * D].rearrange("p (t n) -> p t n", t=4)
             nc.gpsimd.tensor_scalar(
                 out=vg[:].rearrange("p (c i t) -> p c t i", i=4, t=4),
-                in0=v_raw[b][:, g * 4 * D : (g + 1) * 4 * D].rearrange("p (t c i) -> p c t i", t=4, i=4),
+                in0=src[:, :, c * P : (c + 1) * P].rearrange("p t (c i) -> p c t i", i=4),
                 scalar1=1.0, scalar2=0.0, op0=ALU.mult, op1=ALU.add,
             )
-            v_grouped[(b, g)] = vg
+            v_grouped[w] = vg
 
-        def v_quant(b, g):
-            if g == 0:
+        def v_quant(w):
+            b, c0 = w // 8, (w % 8) * P
+            if w % 8 == 0:
                 vw[b] = words.tile([P, 2 * D], U32, name="vw", tag="vw", align_bytes=64)
                 vs[b] = words.tile([P, 2 * D], U8, name="vs", tag="vs", align_bytes=64)
             nc.vector.quantize_mx(
-                out=vw[b][:, g * D : (g + 1) * D].bitcast(FP8X4),
-                scales=vs[b][:, g * D : (g + 1) * D],
-                in_=v_grouped[(b, g)][:],
+                out=vw[b][:, c0 : c0 + P].bitcast(FP8X4), scales=vs[b][:, c0 : c0 + P],
+                in_=v_grouped[w][:],
             )
 
         score_ps, x_sb, neg_max, row_sum, attn_sb, at_ps, at_grouped = {}, {}, {}, {}, {}, {}, {}
@@ -272,19 +278,18 @@ def tile_positionawareattention_pa_t_kernel(tc, q, k, v, out_0, out_1):
                     in_=ctx_sb[n // 2][:].rearrange("p (t d) -> p t d", t=2),
                 )
 
-        first = [0, 1, 4, 5, 2, 3]
+        first = [0, 4, 1, 2, 3, 5]
         for i, u in enumerate(first):
             prep_transpose(0, u, "score" if i < 4 else "at_ps", 5 if i < 4 else 2)
         for i, u in enumerate(first):
             prep_out(0, u, on_vector=(i % 2 == 0))
-            if i == 3:
+            if i == 2:
                 finish_table()
             if i >= 1:
                 prep_quant(0, first[i - 1])
-        prep_quant(0, first[-1])
-        v_regroup(0, 0)
-        v_regroup(0, 1)
         qk(0)
+        for w in range(3):
+            v_regroup(w)
 
         units = [(b, u) for b in range(1, B) for u in range(8)]
 
@@ -298,6 +303,8 @@ def tile_positionawareattention_pa_t_kernel(tc, q, k, v, out_0, out_1):
             late = step >= TILES
             if live(step - 2):
                 normalise(step - 2, on_vector=late)
+            if step + 3 < 8 * B:
+                v_regroup(step + 3)
             if live(step - 4):
                 transpose_attn(step - 4, "score" if late else "at_ps", 5 if late else 2)
             if step in (0, 1):
@@ -311,7 +318,7 @@ def tile_positionawareattention_pa_t_kernel(tc, q, k, v, out_0, out_1):
             if live(step - 1):
                 exponent(step - 1)
             if live(step - 7):
-                ctx_store(step - 7, on_vector=((step - 7) % 4 == 3))
+                ctx_store(step - 7, on_vector=(late or (COUT_V and (step - 7) % COUT_V == 0)))
             if live(step - 6):
                 av(step - 6)
             if live(step - 4):
@@ -324,12 +331,10 @@ def tile_positionawareattention_pa_t_kernel(tc, q, k, v, out_0, out_1):
                 quantise_attn(step - 5)
             if unit(step - 1):
                 prep_quant(unit(step - 1)[0], unit(step - 1)[1])
-            if step in (1, 2):
+            if step in (0, 1, 2):
                 prep_quant(0, 5 + step)
-            if step in (0, 1):
-                v_quant(0, step)
-            for b in range(1, B):
-                if step in (NT * b - 4, NT * b - 2):
-                    v_regroup(b, (step - NT * b + 4) // 2)
-                if step in (NT * b - 1, NT * b + 1):
-                    v_quant(b, (step - NT * b + 1) // 2)
+            if step == 0:
+                v_quant(0)
+                v_quant(1)
+            if step + 2 < 8 * B:
+                v_quant(step + 2)

@@ -25,17 +25,14 @@ P = 128
 NT = S // P
 TILES = B * NT
 BANK = 512
+TABLE = S + NT
 FLOPS = 2 * 2 * B * S * S * D
-
-PINNED = True
-COUT_V = 0
 
 
 def tile_positionawareattention_pa_t_kernel(tc, q, k, v, out_0, out_1):
     nc = tc.nc
     with ExitStack() as ctx:
-        if PINNED:
-            ctx.enter_context(tc.manual_schedule())
+        ctx.enter_context(tc.manual_schedule())
         const = ctx.enter_context(tc.tile_pool(name="const", bufs=1))
         raw = ctx.enter_context(tc.tile_pool(name="raw", bufs=1))
         words = ctx.enter_context(tc.tile_pool(name="words", bufs=2))
@@ -74,33 +71,32 @@ def tile_positionawareattention_pa_t_kernel(tc, q, k, v, out_0, out_1):
             load(q_raw[b], q_view[b], 0, 8)
             load(v_raw[b], v_view[b], 0, 8)
 
-        TW = S + NT
-        d_hi_i = const.tile([P, TW // NT], I32, name="d_hi_i", tag="d_hi_i")
+        d_hi_i = const.tile([P, TABLE // NT], I32, name="d_hi_i", tag="d_hi_i")
         d_lo_i = const.tile([P, NT], I32, name="d_lo_i", tag="d_lo_i")
-        nc.gpsimd.iota(d_hi_i[:], pattern=[[-NT, TW // NT]], base=NT - 1, channel_multiplier=NT)
+        nc.gpsimd.iota(d_hi_i[:], pattern=[[-NT, TABLE // NT]], base=NT - 1, channel_multiplier=NT)
         nc.gpsimd.iota(d_lo_i[:], pattern=[[1, NT]], base=0, channel_multiplier=0)
         ident = const.tile([P, P], F32, name="ident", tag="ident")
         make_identity(nc, ident[:])
-        d_hi = const.tile([P, TW // NT], F32, name="d_hi", tag="d_hi")
+        d_hi = const.tile([P, TABLE // NT], F32, name="d_hi", tag="d_hi")
         d_lo = const.tile([P, NT], F32, name="d_lo", tag="d_lo")
         nc.vector.tensor_copy(out=d_hi[:], in_=d_hi_i[:])
         nc.vector.tensor_copy(out=d_lo[:], in_=d_lo_i[:])
-        dist = const.tile([P, TW], F32, name="dist", tag="dist")
+        dist = const.tile([P, TABLE], F32, name="dist", tag="dist")
         nc.vector.tensor_tensor(
             out=dist[:].rearrange("p (a c) -> p a c", c=NT),
-            in0=d_hi[:].unsqueeze(2).to_broadcast([P, TW // NT, NT]),
-            in1=d_lo[:].unsqueeze(1).to_broadcast([P, TW // NT, NT]),
+            in0=d_hi[:].unsqueeze(2).to_broadcast([P, TABLE // NT, NT]),
+            in1=d_lo[:].unsqueeze(1).to_broadcast([P, TABLE // NT, NT]),
             op=ALU.subtract,
         )
         nc.scalar.activation(out=dist[:], in_=dist[:], func=ACT.Abs)
-        decay = const.tile([P, TW], F32, name="decay", tag="decay")
+        decay = const.tile([P, TABLE], F32, name="decay", tag="decay")
         nc.scalar.activation(out=decay[:], in_=dist[:], func=ACT.Exp, scale=-BETA / S)
-        neg_pw = const.tile([P, TW], F32, name="neg_pw", tag="neg_pw")
-        unit_w = ALPHA / ((1.0 + GAMMA) * math.sqrt(D) * TEMPERATURE)
+        neg_pw = const.tile([P, TABLE], F32, name="neg_pw", tag="neg_pw")
+        far_weight = ALPHA / ((1.0 + GAMMA) * math.sqrt(D) * TEMPERATURE)
 
         def finish_table():
             nc.vector.tensor_scalar(
-                out=neg_pw[:], in0=decay[:], scalar1=-GAMMA * unit_w, scalar2=-unit_w,
+                out=neg_pw[:], in0=decay[:], scalar1=-GAMMA * far_weight, scalar2=-far_weight,
                 op0=ALU.mult, op1=ALU.add,
             )
 
@@ -134,7 +130,7 @@ def tile_positionawareattention_pa_t_kernel(tc, q, k, v, out_0, out_1):
             grouped[(b, u)] = g
 
         def prep_quant(b, u):
-            c0 = 256 * (u % 4)
+            c0 = 2 * P * (u % 4)
             if u == 0:
                 kw[b] = words.tile([P, S], U32, name="kw", tag="kw", align_bytes=64)
                 ks[b] = words.tile([P, S], U8, name="ks", tag="ks", align_bytes=64)
@@ -143,7 +139,7 @@ def tile_positionawareattention_pa_t_kernel(tc, q, k, v, out_0, out_1):
                 qs[b] = words.tile([P, S], U8, name="qs", tag="qs", align_bytes=64)
             w, sc = (kw[b], ks[b]) if u < 4 else (qw[b], qs[b])
             nc.vector.quantize_mx(
-                out=w[:, c0 : c0 + 256].bitcast(FP8X4), scales=sc[:, c0 : c0 + 256],
+                out=w[:, c0 : c0 + 2 * P].bitcast(FP8X4), scales=sc[:, c0 : c0 + 2 * P],
                 in_=grouped[(b, u)][:],
             )
 
@@ -210,26 +206,23 @@ def tile_positionawareattention_pa_t_kernel(tc, q, k, v, out_0, out_1):
             )
             row_sum[n] = sm
 
-        def normalise(n, on_vector):
+        def normalise(n):
             b, t = divmod(n, NT)
             r = small.tile([P, 1], F32, name="recip", tag="recip")
             nc.vector.reciprocal(out=r[:], in_=row_sum[n][:])
             a = attn_sb[n // 2][:, (n % 2) * S : (n % 2 + 1) * S]
-            if on_vector:
-                nc.vector.tensor_scalar_mul(out=a, in0=a, scalar1=r[:])
-            else:
-                nc.gpsimd.tensor_scalar(
-                    out=a, in0=a, scalar1=r[:], scalar2=0.0, op0=ALU.mult, op1=ALU.add
-                )
+            nc.gpsimd.tensor_scalar(
+                out=a, in0=a, scalar1=r[:], scalar2=0.0, op0=ALU.mult, op1=ALU.add
+            )
             if n % 2 == 1:
                 nc.sync.dma_start(
                     out=attn_out[b][:, t - 1 : t + 1, :],
                     in_=attn_sb[n // 2][:].rearrange("p (t j) -> p t j", t=2),
                 )
 
-        def transpose_attn(n, tag, bufs):
+        def transpose_attn(n):
             for g in range(2):
-                ps = psum.tile([P, BANK], F32, name="at_ps", tag=tag, bufs=bufs)
+                ps = psum.tile([P, BANK], F32, name="at_ps", tag="at_ps", bufs=2)
                 for c in range(4):
                     col = (n % 2) * S + (4 * g + c) * P
                     nc.tensor.transpose(
@@ -237,19 +230,18 @@ def tile_positionawareattention_pa_t_kernel(tc, q, k, v, out_0, out_1):
                     )
                 at_ps[(n, g)] = ps
 
-        def regroup_attn(n, shared):
+        def regroup_attn(n):
             gr = stage.tile([P, 1024], BF16, name="at_grouped", tag="at_grouped", align_bytes=64)
             for g in range(2):
-                copy_out(
-                    shared and g == 1,
-                    gr[:, g * BANK : (g + 1) * BANK].rearrange("p (r c) -> p r c", c=4),
-                    at_ps[(n, g)][:].rearrange("p (c r) -> p r c", c=4),
+                nc.scalar.copy(
+                    out=gr[:, g * BANK : (g + 1) * BANK].rearrange("p (r c) -> p r c", c=4),
+                    in_=at_ps[(n, g)][:].rearrange("p (c r) -> p r c", c=4),
                 )
             at_grouped[n] = gr
 
         def quantise_attn(n):
-            w = stage.tile([P, 256], U32, name="at_words", tag="at_words", align_bytes=64)
-            sc = stage.tile([P, 256], U8, name="at_scales", tag="at_scales", align_bytes=64)
+            w = stage.tile([P, 2 * P], U32, name="at_words", tag="at_words", align_bytes=64)
+            sc = stage.tile([P, 2 * P], U8, name="at_scales", tag="at_scales", align_bytes=64)
             nc.vector.quantize_mx(out=w[:].bitcast(FP8X4), scales=sc[:], in_=at_grouped[n][:])
             at_words[n], at_scales[n] = w, sc
 
@@ -267,26 +259,26 @@ def tile_positionawareattention_pa_t_kernel(tc, q, k, v, out_0, out_1):
                 )
             ctx_ps[n] = ps
 
-        def ctx_store(n, on_vector):
+        def ctx_store(n):
             b, t = divmod(n, NT)
             if n % 2 == 0:
                 ctx_sb[n // 2] = work.tile([P, 2 * D], F32, name="ctx_sb", tag="ctx_sb")
-            copy_out(on_vector, ctx_sb[n // 2][:, (n % 2) * D : (n % 2 + 1) * D], ctx_ps[n][:])
+            nc.scalar.copy(out=ctx_sb[n // 2][:, (n % 2) * D : (n % 2 + 1) * D], in_=ctx_ps[n][:])
             if n % 2 == 1:
                 nc.sync.dma_start(
                     out=ctx_out[b][:, t - 1 : t + 1, :],
                     in_=ctx_sb[n // 2][:].rearrange("p (t d) -> p t d", t=2),
                 )
 
-        first = [0, 4, 1, 2, 3, 5]
-        for i, u in enumerate(first):
+        head = [0, 4, 1, 2, 3, 5]
+        for i, u in enumerate(head):
             prep_transpose(0, u, "score" if i < 4 else "at_ps", 5 if i < 4 else 2)
-        for i, u in enumerate(first):
+        for i, u in enumerate(head):
             prep_out(0, u, on_vector=(i % 2 == 0))
             if i == 2:
                 finish_table()
             if i >= 1:
-                prep_quant(0, first[i - 1])
+                prep_quant(0, head[i - 1])
         qk(0)
         for w in range(3):
             v_regroup(w)
@@ -300,13 +292,12 @@ def tile_positionawareattention_pa_t_kernel(tc, q, k, v, out_0, out_1):
             return units[j] if 0 <= j < len(units) else None
 
         for step in range(TILES + 8):
-            late = step >= TILES
             if live(step - 2):
-                normalise(step - 2, on_vector=late)
+                normalise(step - 2)
             if step + 3 < 8 * B:
                 v_regroup(step + 3)
             if live(step - 4):
-                transpose_attn(step - 4, "score" if late else "at_ps", 5 if late else 2)
+                transpose_attn(step - 4)
             if step in (0, 1):
                 prep_transpose(0, 6 + step, "at_ps", 2)
             if unit(step):
@@ -318,11 +309,11 @@ def tile_positionawareattention_pa_t_kernel(tc, q, k, v, out_0, out_1):
             if live(step - 1):
                 exponent(step - 1)
             if live(step - 7):
-                ctx_store(step - 7, on_vector=(late or (COUT_V and (step - 7) % COUT_V == 0)))
+                ctx_store(step - 7)
             if live(step - 6):
                 av(step - 6)
             if live(step - 4):
-                regroup_attn(step - 4, shared=late)
+                regroup_attn(step - 4)
             if step in (0, 1):
                 prep_out(0, 6 + step, on_vector=False)
             if unit(step):

@@ -67,27 +67,15 @@ def tile_positionawareattention_pa_t_kernel(tc, q, k, v, out_0, out_1):
         load(v_raw[0], v_view[0], 0, 4)
         load(v_raw[0], v_view[0], 4, 8)
         for b in range(1, B):
-            load(k_raw[b], k_view[b], 0, 8)
+            load(k_raw[b], k_view[b], 0, 4)
+            load(k_raw[b], k_view[b], 4, 8)
             load(q_raw[b], q_view[b], 0, 8)
             load(v_raw[b], v_view[b], 0, 8)
 
-        d_hi_i = const.tile([P, TABLE // NT], I32, name="d_hi_i", tag="d_hi_i")
-        d_lo_i = const.tile([P, NT], I32, name="d_lo_i", tag="d_lo_i")
-        nc.gpsimd.iota(d_hi_i[:], pattern=[[-NT, TABLE // NT]], base=NT - 1, channel_multiplier=NT)
-        nc.gpsimd.iota(d_lo_i[:], pattern=[[1, NT]], base=0, channel_multiplier=0)
+        dist = const.tile([P, TABLE], F32, name="dist", tag="dist")
+        nc.gpsimd.iota(dist[:], pattern=[[-1, TABLE]], base=NT - 1, channel_multiplier=NT, allow_small_or_imprecise_dtypes=True)
         ident = const.tile([P, P], F32, name="ident", tag="ident")
         make_identity(nc, ident[:])
-        d_hi = const.tile([P, TABLE // NT], F32, name="d_hi", tag="d_hi")
-        d_lo = const.tile([P, NT], F32, name="d_lo", tag="d_lo")
-        nc.vector.tensor_copy(out=d_hi[:], in_=d_hi_i[:])
-        nc.vector.tensor_copy(out=d_lo[:], in_=d_lo_i[:])
-        dist = const.tile([P, TABLE], F32, name="dist", tag="dist")
-        nc.vector.tensor_tensor(
-            out=dist[:].rearrange("p (a c) -> p a c", c=NT),
-            in0=d_hi[:].unsqueeze(2).to_broadcast([P, TABLE // NT, NT]),
-            in1=d_lo[:].unsqueeze(1).to_broadcast([P, TABLE // NT, NT]),
-            op=ALU.subtract,
-        )
         nc.scalar.activation(out=dist[:], in_=dist[:], func=ACT.Abs)
         decay = const.tile([P, TABLE], F32, name="decay", tag="decay")
         nc.scalar.activation(out=decay[:], in_=dist[:], func=ACT.Exp, scale=-BETA / S)
@@ -95,7 +83,7 @@ def tile_positionawareattention_pa_t_kernel(tc, q, k, v, out_0, out_1):
         far_weight = ALPHA / ((1.0 + GAMMA) * math.sqrt(D) * TEMPERATURE)
 
         def finish_table():
-            nc.vector.tensor_scalar(
+            nc.gpsimd.tensor_scalar(
                 out=neg_pw[:], in0=decay[:], scalar1=-GAMMA * far_weight, scalar2=-far_weight,
                 op0=ALU.mult, op1=ALU.add,
             )
@@ -121,7 +109,7 @@ def tile_positionawareattention_pa_t_kernel(tc, q, k, v, out_0, out_1):
             prep_ps[(b, u)] = bank
 
         def prep_out(b, u, on_vector):
-            g = stage.tile([P, 1024], BF16, name="grouped", tag="grouped", bufs=4, align_bytes=64)
+            g = stage.tile([P, 1024], BF16, name="grouped", tag="grouped", bufs=6, align_bytes=64)
             copy_out(
                 on_vector,
                 g[:].bitcast(F32).rearrange("p (s r h) -> p s r h", s=2, h=2),
@@ -145,23 +133,24 @@ def tile_positionawareattention_pa_t_kernel(tc, q, k, v, out_0, out_1):
 
         def v_regroup(w):
             b, g, c = w // 8, (w % 8) // 4, w % 4
-            vg = stage.tile([P, 4 * P], BF16, name="v_grouped", tag="v_grouped", bufs=5, align_bytes=64)
+            if w % 2 == 0:
+                v_grouped[w // 2] = stage.tile([P, 8 * P], BF16, name="v_grouped", tag="v_grouped", bufs=3, align_bytes=64)
+            vg = v_grouped[w // 2][:, (w % 2) * 4 * P : (w % 2 + 1) * 4 * P]
             src = v_raw[b][:, g * 4 * D : (g + 1) * 4 * D].rearrange("p (t n) -> p t n", t=4)
             nc.gpsimd.tensor_scalar(
-                out=vg[:].rearrange("p (c i t) -> p c t i", i=4, t=4),
+                out=vg.rearrange("p (c i t) -> p c t i", i=4, t=4),
                 in0=src[:, :, c * P : (c + 1) * P].rearrange("p t (c i) -> p c t i", i=4),
                 scalar1=1.0, scalar2=0.0, op0=ALU.mult, op1=ALU.add,
             )
-            v_grouped[w] = vg
 
-        def v_quant(w):
-            b, c0 = w // 8, (w % 8) * P
-            if w % 8 == 0:
+        def v_quant(u):
+            b, c0 = u // 4, (u % 4) * 2 * P
+            if u % 4 == 0:
                 vw[b] = words.tile([P, 2 * D], U32, name="vw", tag="vw", align_bytes=64)
                 vs[b] = words.tile([P, 2 * D], U8, name="vs", tag="vs", align_bytes=64)
             nc.vector.quantize_mx(
-                out=vw[b][:, c0 : c0 + P].bitcast(FP8X4), scales=vs[b][:, c0 : c0 + P],
-                in_=v_grouped[w][:],
+                out=vw[b][:, c0 : c0 + 2 * P].bitcast(FP8X4), scales=vs[b][:, c0 : c0 + 2 * P],
+                in_=v_grouped[u][:],
             )
 
         score_ps, x_sb, neg_max, row_sum, attn_sb, at_ps, at_grouped = {}, {}, {}, {}, {}, {}, {}
@@ -170,31 +159,39 @@ def tile_positionawareattention_pa_t_kernel(tc, q, k, v, out_0, out_1):
         ctx_out = [out_0[b].rearrange("(p t) d -> p t d", t=NT) for b in range(B)]
 
         def qk(n):
-            b, t = divmod(n, NT)
             for h in range(2):
-                ps = psum.tile([P, BANK], F32, name="score_ps", tag="score", bufs=5)
-                nc.tensor.matmul_mx(
-                    out=ps[:],
-                    lhsT=qw[b][:, t * P : (t + 1) * P].bitcast(FP8X4),
-                    lhsT_scale=qs[b][:, t * P : (t + 1) * P],
-                    rhs=kw[b][:, h * BANK : (h + 1) * BANK].bitcast(FP8X4),
-                    rhs_scale=ks[b][:, h * BANK : (h + 1) * BANK],
-                    start=True, stop=True,
-                )
-                score_ps[(n, h)] = ps
+                qk_half(n, h)
 
-        def weigh_and_max(n):
-            t = n % NT
-            x = work.tile([P, S], F32, name="x_sb", tag="x_sb")
+        def qk_half(n, h):
+            b, t = divmod(n, NT)
+            ps = psum.tile([P, BANK], F32, name="score_ps", tag="score", bufs=5)
+            nc.tensor.matmul_mx(
+                out=ps[:],
+                lhsT=qw[b][:, t * P : (t + 1) * P].bitcast(FP8X4),
+                lhsT_scale=qs[b][:, t * P : (t + 1) * P],
+                rhs=kw[b][:, h * BANK : (h + 1) * BANK].bitcast(FP8X4),
+                rhs_scale=ks[b][:, h * BANK : (h + 1) * BANK],
+                start=True, stop=True,
+            )
+            score_ps[(n, h)] = ps
+
+        def weigh(n):
             for h in range(2):
-                c0 = NT - 1 - t + h * BANK
-                nc.vector.tensor_tensor(
-                    out=x[:, h * BANK : (h + 1) * BANK], in0=score_ps[(n, h)][:],
-                    in1=neg_pw[:, c0 : c0 + BANK], op=ALU.mult,
-                )
+                weigh_half(n, h)
+
+        def weigh_half(n, h):
+            c0 = NT - 1 - n % NT + h * BANK
+            if h == 0:
+                x_sb[n] = work.tile([P, S], F32, name="x_sb", tag="x_sb")
+            nc.vector.tensor_tensor(
+                out=x_sb[n][:, h * BANK : (h + 1) * BANK], in0=score_ps[(n, h)][:],
+                in1=neg_pw[:, c0 : c0 + BANK], op=ALU.mult,
+            )
+
+        def row_max(n):
             m = small.tile([P, 1], F32, name="neg_max", tag="neg_max")
-            nc.vector.tensor_reduce(out=m[:], in_=x[:], axis=AX.X, op=ALU.min)
-            x_sb[n], neg_max[n] = x, m
+            nc.vector.tensor_reduce(out=m[:], in_=x_sb[n][:], axis=AX.X, op=ALU.min)
+            neg_max[n] = m
 
         def exponent(n):
             if n % 2 == 0:
@@ -206,12 +203,12 @@ def tile_positionawareattention_pa_t_kernel(tc, q, k, v, out_0, out_1):
             )
             row_sum[n] = sm
 
-        def normalise(n):
+        def normalise(n, on_vector=False):
             b, t = divmod(n, NT)
             r = small.tile([P, 1], F32, name="recip", tag="recip")
             nc.vector.reciprocal(out=r[:], in_=row_sum[n][:])
             a = attn_sb[n // 2][:, (n % 2) * S : (n % 2 + 1) * S]
-            nc.gpsimd.tensor_scalar(
+            (nc.vector if on_vector else nc.gpsimd).tensor_scalar(
                 out=a, in0=a, scalar1=r[:], scalar2=0.0, op0=ALU.mult, op1=ALU.add
             )
             if n % 2 == 1:
@@ -230,10 +227,10 @@ def tile_positionawareattention_pa_t_kernel(tc, q, k, v, out_0, out_1):
                     )
                 at_ps[(n, g)] = ps
 
-        def regroup_attn(n):
+        def regroup_attn(n, share=False):
             gr = stage.tile([P, 1024], BF16, name="at_grouped", tag="at_grouped", align_bytes=64)
             for g in range(2):
-                nc.scalar.copy(
+                copy_out(share and g == 1,
                     out=gr[:, g * BANK : (g + 1) * BANK].rearrange("p (r c) -> p r c", c=4),
                     in_=at_ps[(n, g)][:].rearrange("p (c r) -> p r c", c=4),
                 )
@@ -259,27 +256,42 @@ def tile_positionawareattention_pa_t_kernel(tc, q, k, v, out_0, out_1):
                 )
             ctx_ps[n] = ps
 
-        def ctx_store(n):
+        def ctx_store(n, share=False):
             b, t = divmod(n, NT)
             if n % 2 == 0:
                 ctx_sb[n // 2] = work.tile([P, 2 * D], F32, name="ctx_sb", tag="ctx_sb")
-            nc.scalar.copy(out=ctx_sb[n // 2][:, (n % 2) * D : (n % 2 + 1) * D], in_=ctx_ps[n][:])
-            if n % 2 == 1:
+            copy_out(share, out=ctx_sb[n // 2][:, (n % 2) * D : (n % 2 + 1) * D], in_=ctx_ps[n][:])
+            if n >= TILES - 2:
+                nc.sync.dma_start(
+                    out=ctx_out[b][:, t : t + 1, :],
+                    in_=ctx_sb[n // 2][:, (n % 2) * D : (n % 2 + 1) * D].rearrange("p (t d) -> p t d", t=1),
+                )
+            elif n % 2 == 1:
                 nc.sync.dma_start(
                     out=ctx_out[b][:, t - 1 : t + 1, :],
                     in_=ctx_sb[n // 2][:].rearrange("p (t d) -> p t d", t=2),
                 )
 
-        head = [0, 4, 1, 2, 3, 5]
+        finish_table()
+        head = [0, 1, 4, 2, 3, 5]
         for i, u in enumerate(head):
             prep_transpose(0, u, "score" if i < 4 else "at_ps", 5 if i < 4 else 2)
-        for i, u in enumerate(head):
-            prep_out(0, u, on_vector=(i % 2 == 0))
-            if i == 2:
-                finish_table()
-            if i >= 1:
-                prep_quant(0, head[i - 1])
-        qk(0)
+        prep_out(0, 0, True)
+        prep_out(0, 1, True)
+        prep_out(0, 4, False)
+        prep_out(0, 2, False)
+        prep_out(0, 3, False)
+        prep_out(0, 5, False)
+        prep_quant(0, 0)
+        prep_quant(0, 1)
+        prep_quant(0, 4)
+        qk_half(0, 0)
+        weigh_half(0, 0)
+        prep_quant(0, 2)
+        prep_quant(0, 3)
+        qk_half(0, 1)
+        weigh_half(0, 1)
+        row_max(0)
         for w in range(3):
             v_regroup(w)
 
@@ -291,7 +303,7 @@ def tile_positionawareattention_pa_t_kernel(tc, q, k, v, out_0, out_1):
         def unit(j):
             return units[j] if 0 <= j < len(units) else None
 
-        for step in range(TILES + 8):
+        for step in range(TILES):
             if live(step - 2):
                 normalise(step - 2)
             if step + 3 < 8 * B:
@@ -300,12 +312,16 @@ def tile_positionawareattention_pa_t_kernel(tc, q, k, v, out_0, out_1):
                 transpose_attn(step - 4)
             if step in (0, 1):
                 prep_transpose(0, 6 + step, "at_ps", 2)
-            if unit(step):
-                prep_transpose(unit(step)[0], unit(step)[1], "prep", 1)
+            if unit(step - 1):
+                prep_transpose(unit(step - 1)[0], unit(step - 1)[1], "prep", 1)
             if live(step + 1):
                 qk(step + 1)
-            if live(step):
-                weigh_and_max(step)
+            if live(step) and step > 0:
+                weigh(step)
+            if live(step - 5):
+                quantise_attn(step - 5)
+            if live(step) and step > 0:
+                row_max(step)
             if live(step - 1):
                 exponent(step - 1)
             if live(step - 7):
@@ -316,16 +332,44 @@ def tile_positionawareattention_pa_t_kernel(tc, q, k, v, out_0, out_1):
                 regroup_attn(step - 4)
             if step in (0, 1):
                 prep_out(0, 6 + step, on_vector=False)
-            if unit(step):
-                prep_out(unit(step)[0], unit(step)[1], on_vector=False)
-            if live(step - 5):
-                quantise_attn(step - 5)
             if unit(step - 1):
-                prep_quant(unit(step - 1)[0], unit(step - 1)[1])
+                prep_out(unit(step - 1)[0], unit(step - 1)[1], on_vector=False)
+            if unit(step - 2):
+                prep_quant(unit(step - 2)[0], unit(step - 2)[1])
             if step in (0, 1, 2):
                 prep_quant(0, 5 + step)
-            if step == 0:
-                v_quant(0)
-                v_quant(1)
-            if step + 2 < 8 * B:
-                v_quant(step + 2)
+            if step in (1, 2):
+                v_quant(step - 1)
+            if step % 2 == 1 and 2 <= (step + 1) // 2 < 4 * B:
+                v_quant((step + 1) // 2)
+
+        T = TILES
+        normalise(T - 2)
+        exponent(T - 1)
+        transpose_attn(T - 4)
+        av(T - 6)
+        quantise_attn(T - 5)
+        regroup_attn(T - 4, True)
+        ctx_store(T - 7)
+        transpose_attn(T - 3)
+        normalise(T - 1, True)
+        av(T - 5)
+        quantise_attn(T - 4)
+        regroup_attn(T - 3, True)
+        ctx_store(T - 6)
+        transpose_attn(T - 2)
+        av(T - 4)
+        quantise_attn(T - 3)
+        regroup_attn(T - 2, True)
+        ctx_store(T - 5)
+        transpose_attn(T - 1)
+        av(T - 3)
+        quantise_attn(T - 2)
+        regroup_attn(T - 1, True)
+        ctx_store(T - 4)
+        av(T - 2)
+        quantise_attn(T - 1)
+        ctx_store(T - 3)
+        av(T - 1)
+        ctx_store(T - 2)
+        ctx_store(T - 1, True)

@@ -72,10 +72,23 @@ def tile_positionawareattention_pa_t_kernel(tc, q, k, v, out_0, out_1):
             load(q_raw[b], q_view[b], 0, 8)
             load(v_raw[b], v_view[b], 0, 8)
 
-        dist = const.tile([P, TABLE], F32, name="dist", tag="dist")
-        nc.gpsimd.iota(dist[:], pattern=[[-1, TABLE]], base=NT - 1, channel_multiplier=NT, allow_small_or_imprecise_dtypes=True)
+        d_hi_i = const.tile([P, TABLE // NT], I32, name="d_hi_i", tag="d_hi_i")
+        d_lo_i = const.tile([P, NT], I32, name="d_lo_i", tag="d_lo_i")
+        nc.gpsimd.iota(d_hi_i[:], pattern=[[-NT, TABLE // NT]], base=NT - 1, channel_multiplier=NT)
+        nc.gpsimd.iota(d_lo_i[:], pattern=[[1, NT]], base=0, channel_multiplier=0)
         ident = const.tile([P, P], F32, name="ident", tag="ident")
         make_identity(nc, ident[:])
+        d_hi = const.tile([P, TABLE // NT], F32, name="d_hi", tag="d_hi")
+        d_lo = const.tile([P, NT], F32, name="d_lo", tag="d_lo")
+        nc.vector.tensor_copy(out=d_hi[:], in_=d_hi_i[:])
+        nc.vector.tensor_copy(out=d_lo[:], in_=d_lo_i[:])
+        dist = const.tile([P, TABLE], F32, name="dist", tag="dist")
+        nc.vector.tensor_tensor(
+            out=dist[:].rearrange("p (a c) -> p a c", c=NT),
+            in0=d_hi[:].unsqueeze(2).to_broadcast([P, TABLE // NT, NT]),
+            in1=d_lo[:].unsqueeze(1).to_broadcast([P, TABLE // NT, NT]),
+            op=ALU.subtract,
+        )
         nc.scalar.activation(out=dist[:], in_=dist[:], func=ACT.Abs)
         decay = const.tile([P, TABLE], F32, name="decay", tag="decay")
         nc.scalar.activation(out=decay[:], in_=dist[:], func=ACT.Exp, scale=-BETA / S)

@@ -331,9 +331,6 @@ def tile_positionawareattention_pa_t_kernel(tc, q, k, v, out_0, out_1):
                 qk(step + 1)
             if live(step) and step > 0:
                 weigh(step)
-            if live(step - 5):
-                quantise_attn(step - 5)
-            if live(step) and step > 0:
                 row_max(step)
             if live(step - 1):
                 exponent(step - 1)
@@ -347,6 +344,8 @@ def tile_positionawareattention_pa_t_kernel(tc, q, k, v, out_0, out_1):
                 prep_out(0, 6 + step, on_vector=False)
             if unit(step - 1):
                 prep_out(unit(step - 1)[0], unit(step - 1)[1], on_vector=False)
+            if live(step - 5):
+                quantise_attn(step - 5)
             if unit(step - 2):
                 prep_quant(unit(step - 2)[0], unit(step - 2)[1])
             if step in (0, 1, 2):

@@ -151,8 +151,8 @@ def tile_positionawareattention_pa_t_kernel(tc, q, k, v, out_0, out_1):
             vg = v_grouped[w // 2][:, (w % 2) * 4 * P : (w % 2 + 1) * 4 * P]
             src = v_raw[b][:, g * 4 * D : (g + 1) * 4 * D].rearrange("p (t n) -> p t n", t=4)
             nc.gpsimd.tensor_scalar(
-                out=vg.rearrange("p (c i t) -> p c t i", i=4, t=4),
-                in0=src[:, :, c * P : (c + 1) * P].rearrange("p t (c i) -> p c t i", i=4),
+                out=vg.rearrange("p (n t) -> p n t", t=4),
+                in0=src[:, :, c * P : (c + 1) * P].rearrange("p t n -> p n t"),
                 scalar1=1.0, scalar2=0.0, op0=ALU.mult, op1=ALU.add,
             )
 

@@ -41,11 +41,14 @@ def tile_positionawareattention_pa_t_kernel(tc, q, k, v, out_0, out_1):
         small = ctx.enter_context(tc.tile_pool(name="small", bufs=4))
         psum = ctx.enter_context(tc.psum_pool(name="psum", bufs=1))
 
-        q_raw, k_raw, v_raw = [], [], []
-        for b in range(B):
-            q_raw.append(raw.tile([P, NT * D], BF16, name="q_raw%d" % b, tag="q_raw%d" % b))
-            k_raw.append(raw.tile([P, NT * D], BF16, name="k_raw%d" % b, tag="k_raw%d" % b))
-            v_raw.append(raw.tile([P, NT * D], BF16, name="v_raw%d" % b, tag="v_raw%d" % b))
+        q_raw, k_raw, v_raw = {}, {}, {}
+
+        def qk_tiles(b):
+            q_raw[b] = raw.tile([P, NT * D], BF16, name="q_raw", tag="q_raw", bufs=3)
+            k_raw[b] = raw.tile([P, NT * D], BF16, name="k_raw", tag="k_raw", bufs=3)
+
+        def v_tile(b):
+            v_raw[b] = raw.tile([P, NT * D], BF16, name="v_raw", tag="v_raw", bufs=3)
 
         def load(dst, src, t0, t1):
             nc.sync.dma_start(
@@ -57,6 +60,9 @@ def tile_positionawareattention_pa_t_kernel(tc, q, k, v, out_0, out_1):
         k_view = [k[b].rearrange("(t p) d -> p t d", p=P) for b in range(B)]
         v_view = [v[b].rearrange("(t p) d -> p t d", p=P) for b in range(B)]
 
+        for b in range(3):
+            qk_tiles(b)
+            v_tile(b)
         load(k_raw[0], k_view[0], 0, 2)
         load(q_raw[0], q_view[0], 0, 2)
         load(k_raw[0], k_view[0], 2, 4)
@@ -64,13 +70,14 @@ def tile_positionawareattention_pa_t_kernel(tc, q, k, v, out_0, out_1):
         load(k_raw[0], k_view[0], 6, 8)
         load(q_raw[0], q_view[0], 2, 4)
         load(q_raw[0], q_view[0], 4, 8)
+        load(k_raw[1], k_view[1], 0, 4)
+        load(k_raw[1], k_view[1], 4, 8)
         load(v_raw[0], v_view[0], 0, 4)
         load(v_raw[0], v_view[0], 4, 8)
-        for b in range(1, B):
-            load(k_raw[b], k_view[b], 0, 4)
-            load(k_raw[b], k_view[b], 4, 8)
-            load(q_raw[b], q_view[b], 0, 8)
-            load(v_raw[b], v_view[b], 0, 8)
+        load(q_raw[1], q_view[1], 0, 8)
+        load(k_raw[2], k_view[2], 0, 8)
+        load(q_raw[2], q_view[2], 0, 8)
+        load(v_raw[1], v_view[1], 0, 8)
 
         d_hi_i = const.tile([P, TABLE // NT], I32, name="d_hi_i", tag="d_hi_i")
         d_lo_i = const.tile([P, NT], I32, name="d_lo_i", tag="d_lo_i")
@@ -122,7 +129,7 @@ def tile_positionawareattention_pa_t_kernel(tc, q, k, v, out_0, out_1):
             prep_ps[(b, u)] = bank
 
         def prep_out(b, u, on_vector):
-            g = stage.tile([P, 1024], BF16, name="grouped", tag="grouped", bufs=6, align_bytes=64)
+            g = stage.tile([P, 1024], BF16, name="grouped", tag="grouped", bufs=12, align_bytes=64)
             copy_out(
                 on_vector,
                 g[:].bitcast(F32).rearrange("p (s r h) -> p s r h", s=2, h=2),
@@ -195,7 +202,7 @@ def tile_positionawareattention_pa_t_kernel(tc, q, k, v, out_0, out_1):
         def weigh_half(n, h):
             c0 = NT - 1 - n % NT + h * BANK
             if h == 0:
-                x_sb[n] = work.tile([P, S], F32, name="x_sb", tag="x_sb")
+                x_sb[n] = work.tile([P, S], F32, name="x_sb", tag="x_sb", bufs=4)
             nc.vector.tensor_tensor(
                 out=x_sb[n][:, h * BANK : (h + 1) * BANK], in0=score_ps[(n, h)][:],
                 in1=neg_pw[:, c0 : c0 + BANK], op=ALU.mult,
@@ -285,6 +292,28 @@ def tile_positionawareattention_pa_t_kernel(tc, q, k, v, out_0, out_1):
                     in_=ctx_sb[n // 2][:].rearrange("p (t d) -> p t d", t=2),
                 )
 
+        units = [(0, 6), (0, 7)] + [(b, u) for b in range(1, B) for u in range(8)]
+        made, done = [0], [0]
+        for step in range(TILES):
+            more = 3 if step < 4 else 2 if step < 6 else 1 - step % 2
+            done.append(min(done[-1] + (2 if 0 < step < 5 else 1), made[-1]))
+            made.append(min(made[-1] + more, len(units)))
+
+        def prep_no(u):
+            return units.index(u)
+
+        def prep_steps(step):
+            return units[made[step] : made[step + 1]]
+
+        def quant_steps(step):
+            return units[done[step] : done[step + 1]]
+
+        def prep_some(step):
+            for u in prep_steps(step):
+                early = step < 4 and prep_no(u) % 3
+                prep_transpose(u[0], u[1], "at_ps" if early else "prep", 2 if early else 1)
+                prep_out(u[0], u[1], on_vector=False)
+
         finish_table()
         head = [0, 1, 4, 2, 3, 5]
         for i, u in enumerate(head):
@@ -304,33 +333,39 @@ def tile_positionawareattention_pa_t_kernel(tc, q, k, v, out_0, out_1):
         prep_quant(0, 3)
         qk_half(0, 1)
         weigh_half(0, 1)
+        prep_some(0)
+        qk(1)
+        prep_quant(0, 5)
         row_max(0)
         for w in range(3):
             v_regroup(w)
 
-        units = [(b, u) for b in range(1, B) for u in range(8)]
-
         def live(n):
             return 0 <= n < TILES
 
-        def unit(j):
-            return units[j] if 0 <= j < len(units) else None
+        def raw_k3():
+            qk_tiles(3)
+            load(k_raw[3], k_view[3], 0, 8)
+            load(q_raw[3], q_view[3], 0, 8)
 
         for step in range(TILES):
             if live(step - 2):
                 normalise(step - 2)
             if step + 3 < 8 * B:
                 v_regroup(step + 3)
+            if step == 3:
+                raw_k3()
+            if step == 6:
+                load(v_raw[2], v_view[2], 0, 8)
+                v_tile(3)
+                load(v_raw[3], v_view[3], 0, 8)
+            if live(step + 2):
+                qk(step + 2)
             if live(step - 4):
                 transpose_attn(step - 4)
-            if step in (0, 1):
-                prep_transpose(0, 6 + step, "at_ps", 2)
-            if unit(step - 1):
-                prep_transpose(unit(step - 1)[0], unit(step - 1)[1], "prep", 1)
             if live(step + 1):
-                qk(step + 1)
-            if live(step) and step > 0:
-                weigh(step)
+                weigh(step + 1)
+            if step > 0:
                 row_max(step)
             if live(step - 1):
                 exponent(step - 1)
@@ -340,16 +375,12 @@ def tile_positionawareattention_pa_t_kernel(tc, q, k, v, out_0, out_1):
                 av(step - 6)
             if live(step - 4):
                 regroup_attn(step - 4)
-            if step in (0, 1):
-                prep_out(0, 6 + step, on_vector=False)
-            if unit(step - 1):
-                prep_out(unit(step - 1)[0], unit(step - 1)[1], on_vector=False)
+            if step > 0:
+                prep_some(step)
             if live(step - 5):
                 quantise_attn(step - 5)
-            if unit(step - 2):
-                prep_quant(unit(step - 2)[0], unit(step - 2)[1])
-            if step in (0, 1, 2):
-                prep_quant(0, 5 + step)
+            for u in quant_steps(step):
+                prep_quant(u[0], u[1])
             if step in (1, 2):
                 v_quant(step - 1)
             if step % 2 == 1 and 2 <= (step + 1) // 2 < 4 * B:

@@ -157,11 +157,14 @@ def tile_positionawareattention_pa_t_kernel(tc, q, k, v, out_0, out_1):
                 v_grouped[w // 2] = stage.tile([P, 8 * P], BF16, name="v_grouped", tag="v_grouped", bufs=3, align_bytes=64)
             vg = v_grouped[w // 2][:, (w % 2) * 4 * P : (w % 2 + 1) * 4 * P]
             src = v_raw[b][:, g * 4 * D : (g + 1) * 4 * D].rearrange("p (t n) -> p t n", t=4)
-            nc.gpsimd.tensor_scalar(
-                out=vg.rearrange("p (n t) -> p n t", t=4),
-                in0=src[:, :, c * P : (c + 1) * P].rearrange("p t n -> p n t"),
-                scalar1=1.0, scalar2=0.0, op0=ALU.mult, op1=ALU.add,
-            )
+            vg = vg.rearrange("p (n t) -> p n t", t=4)
+            src = src[:, :, c * P : (c + 1) * P].rearrange("p t n -> p n t")
+            if w < 3:
+                nc.scalar.copy(out=vg, in_=src)
+            else:
+                nc.gpsimd.tensor_scalar(
+                    out=vg, in0=src, scalar1=1.0, scalar2=0.0, op0=ALU.mult, op1=ALU.add
+                )
 
         def v_quant(u):
             b, c0 = u // 4, (u % 4) * 2 * P
@@ -295,7 +298,7 @@ def tile_positionawareattention_pa_t_kernel(tc, q, k, v, out_0, out_1):
         units = [(0, 6), (0, 7)] + [(b, u) for b in range(1, B) for u in range(8)]
         made, done = [0], [0]
         for step in range(TILES):
-            more = 3 if step < 4 else 2 if step < 6 else 1 - step % 2
+            more = 4 if step < 4 else 1 - step % 2
             done.append(min(done[-1] + (2 if 0 < step < 5 else 1), made[-1]))
             made.append(min(made[-1] + more, len(units)))
 

@@ -90,21 +90,29 @@ def tile_positionawareattention_pa_t_kernel(tc, q, k, v, out_0, out_1):
         nc.vector.tensor_copy(out=d_hi[:], in_=d_hi_i[:])
         nc.vector.tensor_copy(out=d_lo[:], in_=d_lo_i[:])
         dist = const.tile([P, TABLE], F32, name="dist", tag="dist")
-        nc.vector.tensor_tensor(
-            out=dist[:].rearrange("p (a c) -> p a c", c=NT),
-            in0=d_hi[:].unsqueeze(2).to_broadcast([P, TABLE // NT, NT]),
-            in1=d_lo[:].unsqueeze(1).to_broadcast([P, TABLE // NT, NT]),
-            op=ALU.subtract,
-        )
-        nc.scalar.activation(out=dist[:], in_=dist[:], func=ACT.Abs)
         decay = const.tile([P, TABLE], F32, name="decay", tag="decay")
-        nc.scalar.activation(out=decay[:], in_=dist[:], func=ACT.Exp, scale=-BETA / S)
+        halves = [(0, 65), (65, TABLE // NT)]
+        for a0, a1 in halves:
+            nc.vector.tensor_tensor(
+                out=dist[:, a0 * NT : a1 * NT].rearrange("p (a c) -> p a c", c=NT),
+                in0=d_hi[:, a0:a1].unsqueeze(2).to_broadcast([P, a1 - a0, NT]),
+                in1=d_lo[:].unsqueeze(1).to_broadcast([P, a1 - a0, NT]),
+                op=ALU.subtract,
+            )
+        for a0, a1 in halves:
+            piece = dist[:, a0 * NT : a1 * NT]
+            nc.scalar.activation(out=piece, in_=piece, func=ACT.Abs)
+        for a0, a1 in halves:
+            nc.scalar.activation(
+                out=decay[:, a0 * NT : a1 * NT], in_=dist[:, a0 * NT : a1 * NT], func=ACT.Exp, scale=-BETA / S
+            )
         neg_pw = const.tile([P, TABLE], F32, name="neg_pw", tag="neg_pw")
         far_weight = ALPHA / ((1.0 + GAMMA) * math.sqrt(D) * TEMPERATURE)
 
-        def finish_table():
-            nc.gpsimd.tensor_scalar(
-                out=neg_pw[:], in0=decay[:], scalar1=-GAMMA * far_weight, scalar2=-far_weight,
+        def finish_table(h):
+            c0, c1 = halves[h][0] * NT, halves[h][1] * NT
+            nc.vector.tensor_scalar(
+                out=neg_pw[:, c0:c1], in0=decay[:, c0:c1], scalar1=-GAMMA * far_weight, scalar2=-far_weight,
                 op0=ALU.mult, op1=ALU.add,
             )
 
@@ -159,7 +167,7 @@ def tile_positionawareattention_pa_t_kernel(tc, q, k, v, out_0, out_1):
             src = v_raw[b][:, g * 4 * D : (g + 1) * 4 * D].rearrange("p (t n) -> p t n", t=4)
             vg = vg.rearrange("p (n t) -> p n t", t=4)
             src = src[:, :, c * P : (c + 1) * P].rearrange("p t n -> p n t")
-            if w < 3:
+            if w < 2:
                 nc.scalar.copy(out=vg, in_=src)
             else:
                 nc.gpsimd.tensor_scalar(
@@ -311,34 +319,36 @@ def tile_positionawareattention_pa_t_kernel(tc, q, k, v, out_0, out_1):
         def quant_steps(step):
             return units[done[step] : done[step + 1]]
 
-        def prep_some(step):
-            for u in prep_steps(step):
+        def prep_some(step, lo=0, hi=9):
+            for u in prep_steps(step)[lo:hi]:
                 early = step < 4 and prep_no(u) % 3
                 prep_transpose(u[0], u[1], "at_ps" if early else "prep", 2 if early else 1)
                 prep_out(u[0], u[1], on_vector=False)
 
-        finish_table()
-        head = [0, 1, 4, 2, 3, 5]
+        head = [0, 4, 1, 2, 3, 5]
         for i, u in enumerate(head):
             prep_transpose(0, u, "score" if i < 4 else "at_ps", 5 if i < 4 else 2)
         prep_out(0, 0, True)
-        prep_out(0, 1, True)
-        prep_out(0, 4, False)
+        prep_out(0, 4, True)
+        prep_out(0, 1, False)
         prep_out(0, 2, False)
         prep_out(0, 3, False)
         prep_out(0, 5, False)
         prep_quant(0, 0)
-        prep_quant(0, 1)
         prep_quant(0, 4)
+        finish_table(0)
+        prep_quant(0, 1)
         qk_half(0, 0)
-        weigh_half(0, 0)
         prep_quant(0, 2)
+        prep_some(0, 0, 2)
+        weigh_half(0, 0)
+        finish_table(1)
         prep_quant(0, 3)
         qk_half(0, 1)
-        weigh_half(0, 1)
-        prep_some(0)
-        qk(1)
         prep_quant(0, 5)
+        weigh_half(0, 1)
+        prep_some(0, 2)
+        qk(1)
         row_max(0)
         for w in range(3):
             v_regroup(w)
@@ -373,7 +383,7 @@ def tile_positionawareattention_pa_t_kernel(tc, q, k, v, out_0, out_1):
             if live(step - 1):
                 exponent(step - 1)
             if live(step - 7):
-                ctx_store(step - 7)
+                ctx_store(step - 7, step >= TILES - 2)
             if live(step - 6):
                 av(step - 6)
             if live(step - 4):

@@ -248,9 +248,9 @@ def tile_positionawareattention_pa_t_kernel(tc, q, k, v, out_0, out_1):
                     in_=attn_sb[n // 2][:].rearrange("p (t j) -> p t j", t=2),
                 )
 
-        def transpose_attn(n):
+        def transpose_attn(n, tag="at_ps"):
             for g in range(2):
-                ps = psum.tile([P, BANK], F32, name="at_ps", tag="at_ps", bufs=2)
+                ps = psum.tile([P, BANK], F32, name="at_ps", tag=tag, bufs=5 if tag == "score" else 2)
                 for c in range(4):
                     col = (n % 2) * S + (4 * g + c) * P
                     nc.tensor.transpose(
@@ -258,10 +258,10 @@ def tile_positionawareattention_pa_t_kernel(tc, q, k, v, out_0, out_1):
                     )
                 at_ps[(n, g)] = ps
 
-        def regroup_attn(n, share=False):
+        def regroup_attn(n, vector_banks=()):
             gr = stage.tile([P, 1024], BF16, name="at_grouped", tag="at_grouped", align_bytes=64)
             for g in range(2):
-                copy_out(share and g == 1,
+                copy_out(g in vector_banks,
                     out=gr[:, g * BANK : (g + 1) * BANK].rearrange("p (r c) -> p r c", c=4),
                     in_=at_ps[(n, g)][:].rearrange("p (c r) -> p r c", c=4),
                 )
@@ -383,7 +383,7 @@ def tile_positionawareattention_pa_t_kernel(tc, q, k, v, out_0, out_1):
             if live(step - 1):
                 exponent(step - 1)
             if live(step - 7):
-                ctx_store(step - 7, step >= TILES - 2)
+                ctx_store(step - 7, step % 6 == 0 or step == TILES - 1)
             if live(step - 6):
                 av(step - 6)
             if live(step - 4):
@@ -401,31 +401,31 @@ def tile_positionawareattention_pa_t_kernel(tc, q, k, v, out_0, out_1):
 
         T = TILES
         normalise(T - 2)
+        transpose_attn(T - 4, "score")
+        transpose_attn(T - 3)
         exponent(T - 1)
-        transpose_attn(T - 4)
+        regroup_attn(T - 4, (0, 1))
         av(T - 6)
         quantise_attn(T - 5)
-        regroup_attn(T - 4, True)
         ctx_store(T - 7)
-        transpose_attn(T - 3)
         normalise(T - 1, True)
+        regroup_attn(T - 3, (1,))
+        transpose_attn(T - 2, "score")
         av(T - 5)
-        quantise_attn(T - 4)
-        regroup_attn(T - 3, True)
-        ctx_store(T - 6)
-        transpose_attn(T - 2)
-        av(T - 4)
-        quantise_attn(T - 3)
-        regroup_attn(T - 2, True)
-        ctx_store(T - 5)
         transpose_attn(T - 1)
+        quantise_attn(T - 4)
+        ctx_store(T - 6)
+        quantise_attn(T - 3)
+        regroup_attn(T - 2, (1,))
+        regroup_attn(T - 1, (1,))
+        av(T - 4)
+        ctx_store(T - 5)
         av(T - 3)
         quantise_attn(T - 2)
-        regroup_attn(T - 1, True)
-        ctx_store(T - 4)
-        av(T - 2)
         quantise_attn(T - 1)
-        ctx_store(T - 3)
+        av(T - 2)
         av(T - 1)
+        ctx_store(T - 4)
+        ctx_store(T - 3, True)
         ctx_store(T - 2)
         ctx_store(T - 1, True)

@@ -137,16 +137,17 @@ def tile_positionawareattention_pa_t_kernel(tc, q, k, v, out_0, out_1):
             prep_ps[(b, u)] = bank
 
         def prep_out(b, u, on_vector):
-            g = stage.tile([P, 1024], BF16, name="grouped", tag="grouped", bufs=12, align_bytes=64)
+            if u % 2 == 0:
+                grouped[(b, u // 2)] = stage.tile([P, 2048], BF16, name="grouped", tag="grouped", bufs=7, align_bytes=64)
+            g = grouped[(b, u // 2)][:, (u % 2) * 1024 : (u % 2 + 1) * 1024]
             copy_out(
                 on_vector,
-                g[:].bitcast(F32).rearrange("p (s r h) -> p s r h", s=2, h=2),
+                g.bitcast(F32).rearrange("p (s r h) -> p s r h", s=2, h=2),
                 prep_ps[(b, u)][:].rearrange("p (s h r) -> p s r h", s=2, h=2),
             )
-            grouped[(b, u)] = g
 
-        def prep_quant(b, u):
-            c0 = 2 * P * (u % 4)
+        def prep_quant(b, u, count=1):
+            c0, width = 2 * P * (u % 4), 2 * P * count
             if u == 0:
                 kw[b] = words.tile([P, S], U32, name="kw", tag="kw", align_bytes=64)
                 ks[b] = words.tile([P, S], U8, name="ks", tag="ks", align_bytes=64)
@@ -155,8 +156,8 @@ def tile_positionawareattention_pa_t_kernel(tc, q, k, v, out_0, out_1):
                 qs[b] = words.tile([P, S], U8, name="qs", tag="qs", align_bytes=64)
             w, sc = (kw[b], ks[b]) if u < 4 else (qw[b], qs[b])
             nc.vector.quantize_mx(
-                out=w[:, c0 : c0 + 2 * P].bitcast(FP8X4), scales=sc[:, c0 : c0 + 2 * P],
-                in_=grouped[(b, u)][:],
+                out=w[:, c0 : c0 + width].bitcast(FP8X4), scales=sc[:, c0 : c0 + width],
+                in_=grouped[(b, u // 2)][:, (u % 2) * 1024 : (u % 2 + count) * 1024],
             )
 
         def v_regroup(w):
@@ -307,7 +308,7 @@ def tile_positionawareattention_pa_t_kernel(tc, q, k, v, out_0, out_1):
         made, done = [0], [0]
         for step in range(TILES):
             more = 4 if step < 4 else 1 - step % 2
-            done.append(min(done[-1] + (2 if 0 < step < 5 else 1), made[-1]))
+            done.append(min(done[-1] + (2 if 0 < step < 5 or step > 6 and step % 2 == 1 else 0), made[-1]))
             made.append(min(made[-1] + more, len(units)))
 
         def prep_no(u):
@@ -383,7 +384,7 @@ def tile_positionawareattention_pa_t_kernel(tc, q, k, v, out_0, out_1):
             if live(step - 1):
                 exponent(step - 1)
             if live(step - 7):
-                ctx_store(step - 7, step % 6 == 0 or step == TILES - 1)
+                ctx_store(step - 7, step >= TILES - 2)
             if live(step - 6):
                 av(step - 6)
             if live(step - 4):
@@ -392,8 +393,8 @@ def tile_positionawareattention_pa_t_kernel(tc, q, k, v, out_0, out_1):
                 prep_some(step)
             if live(step - 5):
                 quantise_attn(step - 5)
-            for u in quant_steps(step):
-                prep_quant(u[0], u[1])
+            for u in quant_steps(step)[::2]:
+                prep_quant(u[0], u[1], 2)
             if step in (1, 2):
                 v_quant(step - 1)
             if step % 2 == 1 and 2 <= (step + 1) // 2 < 4 * B:

@@ -50,6 +50,12 @@ def tile_positionawareattention_pa_t_kernel(tc, q, k, v, out_0, out_1):
         def v_tile(b):
             v_raw[b] = raw.tile([P, NT * D], BF16, name="v_raw", tag="v_raw", bufs=3)
 
+        def load_k(b, u0, u1):
+            nc.sync.dma_start(
+                out=k_raw[b][:, u0 * 2 * D : u1 * 2 * D].rearrange("p (u x) -> p u x", x=2 * D),
+                in_=k_view[b][:, u0:u1, :],
+            )
+
         def load(dst, src, t0, t1):
             nc.sync.dma_start(
                 out=dst[:, t0 * D : t1 * D].rearrange("p (t d) -> p t d", d=D),
@@ -57,25 +63,25 @@ def tile_positionawareattention_pa_t_kernel(tc, q, k, v, out_0, out_1):
             )
 
         q_view = [q[b].rearrange("(p t) d -> p t d", t=NT) for b in range(B)]
-        k_view = [k[b].rearrange("(t p) d -> p t d", p=P) for b in range(B)]
+        k_view = [k[b].rearrange("(u p s) d -> p u (s d)", p=P, s=2) for b in range(B)]
         v_view = [v[b].rearrange("(t p) d -> p t d", p=P) for b in range(B)]
 
         for b in range(3):
             qk_tiles(b)
             v_tile(b)
-        load(k_raw[0], k_view[0], 0, 2)
+        load_k(0, 0, 1)
         load(q_raw[0], q_view[0], 0, 2)
-        load(k_raw[0], k_view[0], 2, 4)
-        load(k_raw[0], k_view[0], 4, 6)
-        load(k_raw[0], k_view[0], 6, 8)
+        load_k(0, 1, 2)
+        load_k(0, 2, 3)
+        load_k(0, 3, 4)
         load(q_raw[0], q_view[0], 2, 4)
         load(q_raw[0], q_view[0], 4, 8)
-        load(k_raw[1], k_view[1], 0, 4)
-        load(k_raw[1], k_view[1], 4, 8)
+        load_k(1, 0, 2)
+        load_k(1, 2, 4)
         load(v_raw[0], v_view[0], 0, 4)
         load(v_raw[0], v_view[0], 4, 8)
         load(q_raw[1], q_view[1], 0, 8)
-        load(k_raw[2], k_view[2], 0, 8)
+        load_k(2, 0, 4)
         load(q_raw[2], q_view[2], 0, 8)
         load(v_raw[1], v_view[1], 0, 8)
 
@@ -140,11 +146,18 @@ def tile_positionawareattention_pa_t_kernel(tc, q, k, v, out_0, out_1):
             if u % 2 == 0:
                 grouped[(b, u // 2)] = stage.tile([P, 2048], BF16, name="grouped", tag="grouped", bufs=7, align_bytes=64)
             g = grouped[(b, u // 2)][:, (u % 2) * 1024 : (u % 2 + 1) * 1024]
-            copy_out(
-                on_vector,
-                g.bitcast(F32).rearrange("p (s r h) -> p s r h", s=2, h=2),
-                prep_ps[(b, u)][:].rearrange("p (s h r) -> p s r h", s=2, h=2),
-            )
+            if u < 4:
+                copy_out(
+                    on_vector,
+                    g.bitcast(F32).rearrange("p (r s h) -> p r s h", s=2, h=2),
+                    prep_ps[(b, u)][:].rearrange("p (s h r) -> p r s h", s=2, h=2),
+                )
+            else:
+                copy_out(
+                    on_vector,
+                    g.bitcast(F32).rearrange("p (s r h) -> p s r h", s=2, h=2),
+                    prep_ps[(b, u)][:].rearrange("p (s h r) -> p s r h", s=2, h=2),
+                )
 
         def prep_quant(b, u, count=1):
             c0, width = 2 * P * (u % 4), 2 * P * count
@@ -168,12 +181,9 @@ def tile_positionawareattention_pa_t_kernel(tc, q, k, v, out_0, out_1):
             src = v_raw[b][:, g * 4 * D : (g + 1) * 4 * D].rearrange("p (t n) -> p t n", t=4)
             vg = vg.rearrange("p (n t) -> p n t", t=4)
             src = src[:, :, c * P : (c + 1) * P].rearrange("p t n -> p n t")
-            if w < 2:
-                nc.scalar.copy(out=vg, in_=src)
-            else:
-                nc.gpsimd.tensor_scalar(
-                    out=vg, in0=src, scalar1=1.0, scalar2=0.0, op0=ALU.mult, op1=ALU.add
-                )
+            nc.gpsimd.tensor_scalar(
+                out=vg, in0=src, scalar1=1.0, scalar2=0.0, op0=ALU.mult, op1=ALU.add
+            )
 
         def v_quant(u):
             b, c0 = u // 4, (u % 4) * 2 * P
@@ -359,7 +369,7 @@ def tile_positionawareattention_pa_t_kernel(tc, q, k, v, out_0, out_1):
 
         def raw_k3():
             qk_tiles(3)
-            load(k_raw[3], k_view[3], 0, 8)
+            load_k(3, 0, 4)
             load(q_raw[3], q_view[3], 0, 8)
 
         for step in range(TILES):
@@ -384,7 +394,7 @@ def tile_positionawareattention_pa_t_kernel(tc, q, k, v, out_0, out_1):
             if live(step - 1):
                 exponent(step - 1)
             if live(step - 7):
-                ctx_store(step - 7, step >= TILES - 2)
+                ctx_store(step - 7, step >= TILES - 3)
             if live(step - 6):
                 av(step - 6)
             if live(step - 4):

@@ -175,9 +175,9 @@ def tile_positionawareattention_pa_t_kernel(tc, q, k, v, out_0, out_1):
 
         def v_regroup(w):
             b, g, c = w // 8, (w % 8) // 4, w % 4
-            if w % 2 == 0:
-                v_grouped[w // 2] = stage.tile([P, 8 * P], BF16, name="v_grouped", tag="v_grouped", bufs=3, align_bytes=64)
-            vg = v_grouped[w // 2][:, (w % 2) * 4 * P : (w % 2 + 1) * 4 * P]
+            if w % 4 == 0:
+                v_grouped[w // 4] = stage.tile([P, 4 * D], BF16, name="v_grouped", tag="v_grouped", bufs=2, align_bytes=64)
+            vg = v_grouped[w // 4][:, (w % 4) * 4 * P : (w % 4 + 1) * 4 * P]
             src = v_raw[b][:, g * 4 * D : (g + 1) * 4 * D].rearrange("p (t n) -> p t n", t=4)
             vg = vg.rearrange("p (n t) -> p n t", t=4)
             src = src[:, :, c * P : (c + 1) * P].rearrange("p t n -> p n t")
@@ -186,12 +186,12 @@ def tile_positionawareattention_pa_t_kernel(tc, q, k, v, out_0, out_1):
             )
 
         def v_quant(u):
-            b, c0 = u // 4, (u % 4) * 2 * P
-            if u % 4 == 0:
+            b, c0 = u // 2, (u % 2) * D
+            if u % 2 == 0:
                 vw[b] = words.tile([P, 2 * D], U32, name="vw", tag="vw", align_bytes=64)
                 vs[b] = words.tile([P, 2 * D], U8, name="vs", tag="vs", align_bytes=64)
             nc.vector.quantize_mx(
-                out=vw[b][:, c0 : c0 + 2 * P].bitcast(FP8X4), scales=vs[b][:, c0 : c0 + 2 * P],
+                out=vw[b][:, c0 : c0 + D].bitcast(FP8X4), scales=vs[b][:, c0 : c0 + D],
                 in_=v_grouped[u][:],
             )
 
@@ -395,20 +395,18 @@ def tile_positionawareattention_pa_t_kernel(tc, q, k, v, out_0, out_1):
                 exponent(step - 1)
             if live(step - 7):
                 ctx_store(step - 7, step >= TILES - 3)
-            if live(step - 6):
-                av(step - 6)
             if live(step - 4):
                 regroup_attn(step - 4)
             if step > 0:
                 prep_some(step)
+            if live(step - 6):
+                av(step - 6)
             if live(step - 5):
                 quantise_attn(step - 5)
             for u in quant_steps(step)[::2]:
                 prep_quant(u[0], u[1], 2)
-            if step in (1, 2):
-                v_quant(step - 1)
-            if step % 2 == 1 and 2 <= (step + 1) // 2 < 4 * B:
-                v_quant((step + 1) // 2)
+            if step % 4 == 1:
+                v_quant(step // 4)
 
         T = TILES
         normalise(T - 2)

@@ -253,7 +253,9 @@ def tile_positionawareattention_pa_t_kernel(tc, q, k, v, out_0, out_1):
             (nc.vector if on_vector else nc.gpsimd).tensor_scalar(
                 out=a, in0=a, scalar1=r[:], scalar2=0.0, op0=ALU.mult, op1=ALU.add
             )
-            if n % 2 == 1:
+            if n >= TILES - 4:
+                nc.sync.dma_start(out=attn_out[b][:, t, :], in_=a)
+            elif n % 2 == 1:
                 nc.sync.dma_start(
                     out=attn_out[b][:, t - 1 : t + 1, :],
                     in_=attn_sb[n // 2][:].rearrange("p (t j) -> p t j", t=2),
@@ -303,7 +305,7 @@ def tile_positionawareattention_pa_t_kernel(tc, q, k, v, out_0, out_1):
             if n % 2 == 0:
                 ctx_sb[n // 2] = work.tile([P, 2 * D], F32, name="ctx_sb", tag="ctx_sb")
             copy_out(share, out=ctx_sb[n // 2][:, (n % 2) * D : (n % 2 + 1) * D], in_=ctx_ps[n][:])
-            if n >= TILES - 2:
+            if n >= TILES - 8:
                 nc.sync.dma_start(
                     out=ctx_out[b][:, t : t + 1, :],
                     in_=ctx_sb[n // 2][:, (n % 2) * D : (n % 2 + 1) * D].rearrange("p (t d) -> p t d", t=1),
@@ -394,7 +396,7 @@ def tile_positionawareattention_pa_t_kernel(tc, q, k, v, out_0, out_1):
             if live(step - 1):
                 exponent(step - 1)
             if live(step - 7):
-                ctx_store(step - 7, step >= TILES - 3)
+                ctx_store(step - 7, step >= TILES - 2)
             if live(step - 4):
                 regroup_attn(step - 4)
             if step > 0:
@@ -426,13 +428,13 @@ def tile_positionawareattention_pa_t_kernel(tc, q, k, v, out_0, out_1):
         ctx_store(T - 6)
         quantise_attn(T - 3)
         regroup_attn(T - 2, (1,))
+        quantise_attn(T - 2)
         regroup_attn(T - 1, (1,))
         av(T - 4)
         ctx_store(T - 5)
         av(T - 3)
-        quantise_attn(T - 2)
-        quantise_attn(T - 1)
         av(T - 2)
+        quantise_attn(T - 1)
         av(T - 1)
         ctx_store(T - 4)
         ctx_store(T - 3, True)

@@ -77,10 +77,10 @@ def tile_positionawareattention_pa_t_kernel(tc, q, k, v, out_0, out_1):
         load(q_raw[0], q_view[0], 2, 4)
         load(q_raw[0], q_view[0], 4, 8)
         load_k(1, 0, 2)
-        load_k(1, 2, 4)
         load(v_raw[0], v_view[0], 0, 4)
-        load(v_raw[0], v_view[0], 4, 8)
+        load_k(1, 2, 4)
         load(q_raw[1], q_view[1], 0, 8)
+        load(v_raw[0], v_view[0], 4, 8)
         load_k(2, 0, 4)
         load(q_raw[2], q_view[2], 0, 8)
         load(v_raw[1], v_view[1], 0, 8)
@@ -349,19 +349,19 @@ def tile_positionawareattention_pa_t_kernel(tc, q, k, v, out_0, out_1):
         prep_out(0, 5, False)
         prep_quant(0, 0)
         prep_quant(0, 4)
-        finish_table(0)
         prep_quant(0, 1)
         qk_half(0, 0)
+        finish_table(0)
         prep_quant(0, 2)
-        prep_some(0, 0, 2)
-        weigh_half(0, 0)
-        finish_table(1)
         prep_quant(0, 3)
         qk_half(0, 1)
+        prep_some(0, 0, 2)
+        qk(1)
+        weigh_half(0, 0)
+        finish_table(1)
         prep_quant(0, 5)
         weigh_half(0, 1)
         prep_some(0, 2)
-        qk(1)
         row_max(0)
         for w in range(3):
             v_regroup(w)
@@ -428,13 +428,13 @@ def tile_positionawareattention_pa_t_kernel(tc, q, k, v, out_0, out_1):
         ctx_store(T - 6)
         quantise_attn(T - 3)
         regroup_attn(T - 2, (1,))
-        quantise_attn(T - 2)
         regroup_attn(T - 1, (1,))
         av(T - 4)
         ctx_store(T - 5)
         av(T - 3)
-        av(T - 2)
+        quantise_attn(T - 2)
         quantise_attn(T - 1)
+        av(T - 2)
         av(T - 1)
         ctx_store(T - 4)
         ctx_store(T - 3, True)

from contextlib import ExitStack
import math

import concourse.mybir as mybir
from concourse.masks import make_identity

FP8X4 = mybir.dt.float8_e4m3fn_x4
F32 = mybir.dt.float32
BF16 = mybir.dt.bfloat16
U32 = mybir.dt.uint32
U8 = mybir.dt.uint8
I32 = mybir.dt.int32
ACT = mybir.ActivationFunctionType
ALU = mybir.AluOpType
AX = mybir.AxisListType

B = 4
S = 1024
D = 512
ALPHA = 1.0
BETA = 2.0
GAMMA = 1.5
TEMPERATURE = 1.0
P = 128
NT = S // P
TILES = B * NT
BANK = 512
TABLE = S + NT
FLOPS = 2 * 2 * B * S * S * D


def tile_positionawareattention_pa_t_kernel(tc, q, k, v, out_0, out_1):
    nc = tc.nc
    with ExitStack() as ctx:
        ctx.enter_context(tc.manual_schedule())
        const = ctx.enter_context(tc.tile_pool(name="const", bufs=1))
        raw = ctx.enter_context(tc.tile_pool(name="raw", bufs=1))
        words = ctx.enter_context(tc.tile_pool(name="words", bufs=2))
        stage = ctx.enter_context(tc.tile_pool(name="stage", bufs=3))
        work = ctx.enter_context(tc.tile_pool(name="work", bufs=3))
        small = ctx.enter_context(tc.tile_pool(name="small", bufs=4))
        psum = ctx.enter_context(tc.psum_pool(name="psum", bufs=1))

        q_raw, k_raw, v_raw = {}, {}, {}

        def qk_tiles(b):
            q_raw[b] = raw.tile([P, NT * D], BF16, name="q_raw", tag="q_raw", bufs=3)
            k_raw[b] = raw.tile([P, NT * D], BF16, name="k_raw", tag="k_raw", bufs=3)

        def v_tile(b):
            v_raw[b] = raw.tile([P, NT * D], BF16, name="v_raw", tag="v_raw", bufs=3)

        def load_k(b, u0, u1):
            nc.sync.dma_start(
                out=k_raw[b][:, u0 * 2 * D : u1 * 2 * D].rearrange("p (u x) -> p u x", x=2 * D),
                in_=k_view[b][:, u0:u1, :],
            )

        def load(dst, src, t0, t1):
            nc.sync.dma_start(
                out=dst[:, t0 * D : t1 * D].rearrange("p (t d) -> p t d", d=D),
                in_=src[:, t0:t1, :],
            )

        q_view = [q[b].rearrange("(p t) d -> p t d", t=NT) for b in range(B)]
        k_view = [k[b].rearrange("(u p s) d -> p u (s d)", p=P, s=2) for b in range(B)]
        v_view = [v[b].rearrange("(t p) d -> p t d", p=P) for b in range(B)]

        for b in range(3):
            qk_tiles(b)
            v_tile(b)
        load_k(0, 0, 1)
        load(q_raw[0], q_view[0], 0, 2)
        load_k(0, 1, 2)
        load_k(0, 2, 3)
        load_k(0, 3, 4)
        load(q_raw[0], q_view[0], 2, 4)
        load(q_raw[0], q_view[0], 4, 8)
        load_k(1, 0, 2)
        load(v_raw[0], v_view[0], 0, 4)
        load_k(1, 2, 4)
        load(q_raw[1], q_view[1], 0, 8)
        load(v_raw[0], v_view[0], 4, 8)
        load_k(2, 0, 4)
        load(q_raw[2], q_view[2], 0, 8)
        load(v_raw[1], v_view[1], 0, 8)

        d_hi_i = const.tile([P, TABLE // NT], I32, name="d_hi_i", tag="d_hi_i")
        d_lo_i = const.tile([P, NT], I32, name="d_lo_i", tag="d_lo_i")
        nc.gpsimd.iota(d_hi_i[:], pattern=[[-NT, TABLE // NT]], base=NT - 1, channel_multiplier=NT)
        nc.gpsimd.iota(d_lo_i[:], pattern=[[1, NT]], base=0, channel_multiplier=0)
        ident = const.tile([P, P], F32, name="ident", tag="ident")
        make_identity(nc, ident[:])
        d_hi = const.tile([P, TABLE // NT], F32, name="d_hi", tag="d_hi")
        d_lo = const.tile([P, NT], F32, name="d_lo", tag="d_lo")
        nc.vector.tensor_copy(out=d_hi[:], in_=d_hi_i[:])
        nc.vector.tensor_copy(out=d_lo[:], in_=d_lo_i[:])
        dist = const.tile([P, TABLE], F32, name="dist", tag="dist")
        decay = const.tile([P, TABLE], F32, name="decay", tag="decay")
        halves = [(0, 65), (65, TABLE // NT)]
        for a0, a1 in halves:
            nc.vector.tensor_tensor(
                out=dist[:, a0 * NT : a1 * NT].rearrange("p (a c) -> p a c", c=NT),
                in0=d_hi[:, a0:a1].unsqueeze(2).to_broadcast([P, a1 - a0, NT]),
                in1=d_lo[:].unsqueeze(1).to_broadcast([P, a1 - a0, NT]),
                op=ALU.subtract,
            )
        for a0, a1 in halves:
            piece = dist[:, a0 * NT : a1 * NT]
            nc.scalar.activation(out=piece, in_=piece, func=ACT.Abs)
        for a0, a1 in halves:
            nc.scalar.activation(
                out=decay[:, a0 * NT : a1 * NT], in_=dist[:, a0 * NT : a1 * NT], func=ACT.Exp, scale=-BETA / S
            )
        neg_pw = const.tile([P, TABLE], F32, name="neg_pw", tag="neg_pw")
        far_weight = ALPHA / ((1.0 + GAMMA) * math.sqrt(D) * TEMPERATURE)

        def finish_table(h):
            c0, c1 = halves[h][0] * NT, halves[h][1] * NT
            nc.vector.tensor_scalar(
                out=neg_pw[:, c0:c1], in0=decay[:, c0:c1], scalar1=-GAMMA * far_weight, scalar2=-far_weight,
                op0=ALU.mult, op1=ALU.add,
            )

        qw, qs, kw, ks, vw, vs = {}, {}, {}, {}, {}, {}
        prep_ps, grouped, v_grouped = {}, {}, {}

        def copy_out(on_vector, out, in_):
            if on_vector:
                nc.vector.tensor_copy(out=out, in_=in_)
            else:
                nc.scalar.copy(out=out, in_=in_)

        def prep_transpose(b, u, tag, bufs):
            src = (k_raw[b] if u < 4 else q_raw[b])[:].bitcast(F32)
            bank = psum.tile([P, BANK], F32, name="prep_ps", tag=tag, bufs=bufs)
            for s in range(2):
                for h in range(2):
                    col = (2 * (u % 4) + s) * (D // 2) + h * P
                    nc.tensor.transpose(
                        bank[:, (2 * s + h) * P : (2 * s + h + 1) * P], src[:, col : col + P], ident[:]
                    )
            prep_ps[(b, u)] = bank

        def prep_out(b, u, on_vector):
            if u % 2 == 0:
                grouped[(b, u // 2)] = stage.tile([P, 2048], BF16, name="grouped", tag="grouped", bufs=7, align_bytes=64)
            g = grouped[(b, u // 2)][:, (u % 2) * 1024 : (u % 2 + 1) * 1024]
            if u < 4:
                copy_out(
                    on_vector,
                    g.bitcast(F32).rearrange("p (r s h) -> p r s h", s=2, h=2),
                    prep_ps[(b, u)][:].rearrange("p (s h r) -> p r s h", s=2, h=2),
                )
            else:
                copy_out(
                    on_vector,
                    g.bitcast(F32).rearrange("p (s r h) -> p s r h", s=2, h=2),
                    prep_ps[(b, u)][:].rearrange("p (s h r) -> p s r h", s=2, h=2),
                )

        def prep_quant(b, u, count=1):
            c0, width = 2 * P * (u % 4), 2 * P * count
            if u == 0:
                kw[b] = words.tile([P, S], U32, name="kw", tag="kw", align_bytes=64)
                ks[b] = words.tile([P, S], U8, name="ks", tag="ks", align_bytes=64)
            if u == 4:
                qw[b] = words.tile([P, S], U32, name="qw", tag="qw", align_bytes=64)
                qs[b] = words.tile([P, S], U8, name="qs", tag="qs", align_bytes=64)
            w, sc = (kw[b], ks[b]) if u < 4 else (qw[b], qs[b])
            nc.vector.quantize_mx(
                out=w[:, c0 : c0 + width].bitcast(FP8X4), scales=sc[:, c0 : c0 + width],
                in_=grouped[(b, u // 2)][:, (u % 2) * 1024 : (u % 2 + count) * 1024],
            )

        def v_regroup(w):
            b, g, c = w // 8, (w % 8) // 4, w % 4
            if w % 4 == 0:
                v_grouped[w // 4] = stage.tile([P, 4 * D], BF16, name="v_grouped", tag="v_grouped", bufs=2, align_bytes=64)
            vg = v_grouped[w // 4][:, (w % 4) * 4 * P : (w % 4 + 1) * 4 * P]
            src = v_raw[b][:, g * 4 * D : (g + 1) * 4 * D].rearrange("p (t n) -> p t n", t=4)
            vg = vg.rearrange("p (n t) -> p n t", t=4)
            src = src[:, :, c * P : (c + 1) * P].rearrange("p t n -> p n t")
            nc.gpsimd.tensor_scalar(
                out=vg, in0=src, scalar1=1.0, scalar2=0.0, op0=ALU.mult, op1=ALU.add
            )

        def v_quant(u):
            b, c0 = u // 2, (u % 2) * D
            if u % 2 == 0:
                vw[b] = words.tile([P, 2 * D], U32, name="vw", tag="vw", align_bytes=64)
                vs[b] = words.tile([P, 2 * D], U8, name="vs", tag="vs", align_bytes=64)
            nc.vector.quantize_mx(
                out=vw[b][:, c0 : c0 + D].bitcast(FP8X4), scales=vs[b][:, c0 : c0 + D],
                in_=v_grouped[u][:],
            )

        score_ps, x_sb, neg_max, row_sum, attn_sb, at_ps, at_grouped = {}, {}, {}, {}, {}, {}, {}
        at_words, at_scales, ctx_ps, ctx_sb = {}, {}, {}, {}
        attn_out = [out_1[b].rearrange("(p t) j -> p t j", t=NT) for b in range(B)]
        ctx_out = [out_0[b].rearrange("(p t) d -> p t d", t=NT) for b in range(B)]

        def qk(n):
            for h in range(2):
                qk_half(n, h)

        def qk_half(n, h):
            b, t = divmod(n, NT)
            ps = psum.tile([P, BANK], F32, name="score_ps", tag="score", bufs=5)
            nc.tensor.matmul_mx(
                out=ps[:],
                lhsT=qw[b][:, t * P : (t + 1) * P].bitcast(FP8X4),
                lhsT_scale=qs[b][:, t * P : (t + 1) * P],
                rhs=kw[b][:, h * BANK : (h + 1) * BANK].bitcast(FP8X4),
                rhs_scale=ks[b][:, h * BANK : (h + 1) * BANK],
                start=True, stop=True,
            )
            score_ps[(n, h)] = ps

        def weigh(n):
            for h in range(2):
                weigh_half(n, h)

        def weigh_half(n, h):
            c0 = NT - 1 - n % NT + h * BANK
            if h == 0:
                x_sb[n] = work.tile([P, S], F32, name="x_sb", tag="x_sb", bufs=4)
            nc.vector.tensor_tensor(
                out=x_sb[n][:, h * BANK : (h + 1) * BANK], in0=score_ps[(n, h)][:],
                in1=neg_pw[:, c0 : c0 + BANK], op=ALU.mult,
            )

        def row_max(n):
            m = small.tile([P, 1], F32, name="neg_max", tag="neg_max")
            nc.vector.tensor_reduce(out=m[:], in_=x_sb[n][:], axis=AX.X, op=ALU.min)
            neg_max[n] = m

        def exponent(n):
            if n % 2 == 0:
                attn_sb[n // 2] = work.tile([P, 2 * S], F32, name="attn_sb", tag="attn_sb", bufs=4)
            sm = small.tile([P, 1], F32, name="row_sum", tag="row_sum")
            nc.scalar.activation(
                out=attn_sb[n // 2][:, (n % 2) * S : (n % 2 + 1) * S], in_=x_sb[n][:], func=ACT.Exp,
                bias=neg_max[n][:], scale=-1.0, accum_out=sm[:],
            )
            row_sum[n] = sm

        def normalise(n, on_vector=False):
            b, t = divmod(n, NT)
            r = small.tile([P, 1], F32, name="recip", tag="recip")
            nc.vector.reciprocal(out=r[:], in_=row_sum[n][:])
            a = attn_sb[n // 2][:, (n % 2) * S : (n % 2 + 1) * S]
            (nc.vector if on_vector else nc.gpsimd).tensor_scalar(
                out=a, in0=a, scalar1=r[:], scalar2=0.0, op0=ALU.mult, op1=ALU.add
            )
            if n >= TILES - 4:
                nc.sync.dma_start(out=attn_out[b][:, t, :], in_=a)
            elif n % 2 == 1:
                nc.sync.dma_start(
                    out=attn_out[b][:, t - 1 : t + 1, :],
                    in_=attn_sb[n // 2][:].rearrange("p (t j) -> p t j", t=2),
                )

        def transpose_attn(n, tag="at_ps"):
            for g in range(2):
                ps = psum.tile([P, BANK], F32, name="at_ps", tag=tag, bufs=5 if tag == "score" else 2)
                for c in range(4):
                    col = (n % 2) * S + (4 * g + c) * P
                    nc.tensor.transpose(
                        ps[:, c * P : (c + 1) * P], attn_sb[n // 2][:, col : col + P], ident[:]
                    )
                at_ps[(n, g)] = ps

        def regroup_attn(n, vector_banks=()):
            gr = stage.tile([P, 1024], BF16, name="at_grouped", tag="at_grouped", align_bytes=64)
            for g in range(2):
                copy_out(g in vector_banks,
                    out=gr[:, g * BANK : (g + 1) * BANK].rearrange("p (r c) -> p r c", c=4),
                    in_=at_ps[(n, g)][:].rearrange("p (c r) -> p r c", c=4),
                )
            at_grouped[n] = gr

        def quantise_attn(n):
            w = stage.tile([P, 2 * P], U32, name="at_words", tag="at_words", align_bytes=64)
            sc = stage.tile([P, 2 * P], U8, name="at_scales", tag="at_scales", align_bytes=64)
            nc.vector.quantize_mx(out=w[:].bitcast(FP8X4), scales=sc[:], in_=at_grouped[n][:])
            at_words[n], at_scales[n] = w, sc

        def av(n):
            b = n // NT
            ps = psum.tile([P, BANK], F32, name="ctx_ps", tag="score", bufs=5)
            for g in range(2):
                nc.tensor.matmul_mx(
                    out=ps[:],
                    lhsT=at_words[n][:, g * P : (g + 1) * P].bitcast(FP8X4),
                    lhsT_scale=at_scales[n][:, g * P : (g + 1) * P],
                    rhs=vw[b][:, g * D : (g + 1) * D].bitcast(FP8X4),
                    rhs_scale=vs[b][:, g * D : (g + 1) * D],
                    start=(g == 0), stop=(g == 1),
                )
            ctx_ps[n] = ps

        def ctx_store(n, share=False):
            b, t = divmod(n, NT)
            if n % 2 == 0:
                ctx_sb[n // 2] = work.tile([P, 2 * D], F32, name="ctx_sb", tag="ctx_sb")
            copy_out(share, out=ctx_sb[n // 2][:, (n % 2) * D : (n % 2 + 1) * D], in_=ctx_ps[n][:])
            if n >= TILES - 8:
                nc.sync.dma_start(
                    out=ctx_out[b][:, t : t + 1, :],
                    in_=ctx_sb[n // 2][:, (n % 2) * D : (n % 2 + 1) * D].rearrange("p (t d) -> p t d", t=1),
                )
            elif n % 2 == 1:
                nc.sync.dma_start(
                    out=ctx_out[b][:, t - 1 : t + 1, :],
                    in_=ctx_sb[n // 2][:].rearrange("p (t d) -> p t d", t=2),
                )

        units = [(0, 6), (0, 7)] + [(b, u) for b in range(1, B) for u in range(8)]
        made, done = [0], [0]
        for step in range(TILES):
            more = 4 if step < 4 else 1 - step % 2
            done.append(min(done[-1] + (2 if 0 < step < 5 or step > 6 and step % 2 == 1 else 0), made[-1]))
            made.append(min(made[-1] + more, len(units)))

        def prep_no(u):
            return units.index(u)

        def prep_steps(step):
            return units[made[step] : made[step + 1]]

        def quant_steps(step):
            return units[done[step] : done[step + 1]]

        def prep_some(step, lo=0, hi=9):
            for u in prep_steps(step)[lo:hi]:
                early = step < 4 and prep_no(u) % 3
                prep_transpose(u[0], u[1], "at_ps" if early else "prep", 2 if early else 1)
                prep_out(u[0], u[1], on_vector=False)

        head = [0, 4, 1, 2, 3, 5]
        for i, u in enumerate(head):
            prep_transpose(0, u, "score" if i < 4 else "at_ps", 5 if i < 4 else 2)
        prep_out(0, 0, True)
        prep_out(0, 4, True)
        prep_out(0, 1, False)
        prep_out(0, 2, False)
        prep_out(0, 3, False)
        prep_out(0, 5, False)
        prep_quant(0, 0)
        prep_quant(0, 4)
        prep_quant(0, 1)
        qk_half(0, 0)
        finish_table(0)
        prep_quant(0, 2)
        prep_quant(0, 3)
        qk_half(0, 1)
        prep_some(0, 0, 2)
        qk(1)
        weigh_half(0, 0)
        finish_table(1)
        prep_quant(0, 5)
        weigh_half(0, 1)
        prep_some(0, 2)
        row_max(0)
        for w in range(3):
            v_regroup(w)

        def live(n):
            return 0 <= n < TILES

        def raw_k3():
            qk_tiles(3)
            load_k(3, 0, 4)
            load(q_raw[3], q_view[3], 0, 8)

        for step in range(TILES):
            if live(step - 2):
                normalise(step - 2)
            if step + 3 < 8 * B:
                v_regroup(step + 3)
            if step == 3:
                raw_k3()
            if step == 6:
                load(v_raw[2], v_view[2], 0, 8)
                v_tile(3)
                load(v_raw[3], v_view[3], 0, 8)
            if live(step + 2):
                qk(step + 2)
            if live(step - 4):
                transpose_attn(step - 4)
            if live(step + 1):
                weigh(step + 1)
            if step > 0:
                row_max(step)
            if live(step - 1):
                exponent(step - 1)
            if live(step - 7):
                ctx_store(step - 7, step >= TILES - 2)
            if live(step - 4):
                regroup_attn(step - 4)
            if step > 0:
                prep_some(step)
            if live(step - 6):
                av(step - 6)
            if live(step - 5):
                quantise_attn(step - 5)
            for u in quant_steps(step)[::2]:
                prep_quant(u[0], u[1], 2)
            if step % 4 == 1:
                v_quant(step // 4)

        T = TILES
        normalise(T - 2)
        transpose_attn(T - 4, "score")
        transpose_attn(T - 3)
        exponent(T - 1)
        regroup_attn(T - 4, (0, 1))
        av(T - 6)
        quantise_attn(T - 5)
        ctx_store(T - 7)
        normalise(T - 1, True)
        regroup_attn(T - 3, (1,))
        transpose_attn(T - 2, "score")
        av(T - 5)
        transpose_attn(T - 1)
        quantise_attn(T - 4)
        ctx_store(T - 6)
        quantise_attn(T - 3)
        regroup_attn(T - 2, (1,))
        regroup_attn(T - 1, (1,))
        av(T - 4)
        ctx_store(T - 5)
        av(T - 3)
        quantise_attn(T - 2)
        quantise_attn(T - 1)
        av(T - 2)
        av(T - 1)
        ctx_store(T - 4)
        ctx_store(T - 3, True)
        ctx_store(T - 2)
        ctx_store(T - 1, True)
